import numpy as np
import ml_dtypes


def mxq(x, axis, fmt="e4m3"):
    dtype, down = {"e4m3": (ml_dtypes.float8_e4m3fn, 7), "e5m2": (ml_dtypes.float8_e5m2, 14)}[fmt]
    v = np.moveaxis(np.asarray(x, np.float32).astype(ml_dtypes.bfloat16).astype(np.float64), axis, -1)
    blocks = v.reshape(v.shape[:-1] + (-1, 32))
    amax = np.abs(blocks).max(-1, keepdims=True)
    byte = np.maximum(np.where(amax > 0, np.frexp(amax)[1] - 1 + 127, 0) - down, 1)
    scale = np.exp2(byte - 127.0)
    codes = (blocks / scale).astype(np.float32).astype(dtype).astype(np.float64)
    return np.moveaxis((codes * scale).reshape(v.shape), -1, axis)


WIDE = False


def mx_kscale(k):
    if not WIDE:
        return np.ones(k)
    levels = np.array([18, -18])
    if k % 512:
        return np.exp2(np.random.permutation(np.resize(levels, k // 32))).repeat(32)
    a = np.empty((k // 512, 16))
    for p in range(k // 512):
        a[p, :8] = np.random.permutation(np.resize(levels, 8))
        for g in range(8):
            far = levels[np.abs(levels - a[p, g]) >= 10]
            a[p, g + 8] = far[np.random.randint(len(far))]
    return np.exp2(a.ravel()).repeat(32)


BF16 = ml_dtypes.bfloat16


def bf(x):
    return np.asarray(x, np.float32).astype(BF16)


def f64(x):
    return np.asarray(x).astype(np.float64)


N, C, D, H, W, GD, GH, GW = 2, 512, 8, 16, 8, 8, 8, 8
V = D * H * W
G = GD * GH * GW
PD, PH, PW = D // GD, H // GH, W // GW
P = PD * PH * PW
T = N * P * G


def erf(z):
    a = np.minimum(np.abs(z), 6.0)
    q = 2.0 * a * a
    t = a.copy()
    s = a.copy()
    n = 0
    while np.any(t > 1e-18 * s):
        n += 1
        t = t * q / (2 * n + 1)
        s = s + t
    return np.sign(z) * (2.0 / np.sqrt(np.pi)) * np.exp(-a * a) * s


def gelu(t):
    return 0.5 * t * (1.0 + erf(t / np.sqrt(2.0)))


def dgelu(t):
    return 0.5 * (1.0 + erf(t / np.sqrt(2.0))) + t * np.exp(-0.5 * t * t) / np.sqrt(2.0 * np.pi)


def block(t, ps):
    n, c, d, h, w = t.shape
    t = t.reshape(n, c, d // ps[0], ps[0], h // ps[1], ps[1], w // ps[2], ps[2])
    return t.transpose(0, 1, 2, 4, 6, 3, 5, 7).reshape(n, c, -1, ps[0] * ps[1] * ps[2])


def unblock(t, gs, ps):
    n, c = t.shape[:2]
    t = t.reshape(n, c, gs[0], gs[1], gs[2], ps[0], ps[1], ps[2]).transpose(0, 1, 2, 5, 3, 6, 4, 7)
    return t.reshape(n, c, gs[0] * ps[0], gs[1] * ps[1], gs[2] * ps[2])


def to_tokens(t):
    return block(t, (PD, PH, PW)).transpose(1, 0, 3, 2).reshape(C, T)


def from_tokens(t):
    return unblock(t.reshape(C, N, P, G).transpose(1, 0, 3, 2), (GD, GH, GW), (PD, PH, PW))


def setup_inputs():
    u = mx_kscale(G)
    v = mx_kscale(C)
    sc = mx_kscale(G)
    sp = np.clip(mx_kscale(T).reshape(N, P, G)[:, :, 0], 0.125, 8.0)
    gs, ps = (GD, GH, GW), (PD, PH, PW)
    s = unblock(sp[:, None, None, :] * sc[None, None, :, None], gs, ps)
    ug = unblock(u[None, None, :, None] / sp[:, None, None, :], gs, ps)
    x0 = bf(np.random.standard_normal((N, C, D, H, W)))
    w1_0 = bf(np.random.standard_normal((C, C)) / np.sqrt(C))
    b1 = bf(np.random.standard_normal(C) * 0.3)
    w2_0 = bf(np.random.standard_normal((G, G)) / np.sqrt(G))
    b2 = bf(np.random.standard_normal(G) * 0.3)
    g = bf(np.random.standard_normal((N, C, D, H, W)) * np.exp2(np.random.randint(-6, 1, (N, 1, D, H, W)))
           * ug * v[None, :, None, None, None])
    z = (f64(w1_0) @ f64(x0).reshape(N, C, V) + f64(b1)[None, :, None]).reshape(N, C, D, H, W)
    return {"x_norm": bf(f64(x0) * s),
            "w1_u": bf(f64(w1_0) / v[:, None]),
            "b1_u": b1,
            "w2": bf(f64(w2_0) / u[:, None] / sc[None, :]),
            "b2": b2,
            "z": np.asarray(z, np.float32),
            "grad_out": g}


def reference(x_norm, w1_u, b1_u, w2, b2, z, grad_out):
    gy = to_tokens(f64(grad_out)).reshape(C * N * P, G)
    du = (mxq(gy, 1, "e5m2") @ mxq(f64(w2), 0, "e4m3")).reshape(C, T)
    dz = du * dgelu(to_tokens(f64(z)))
    dx = mxq(f64(w1_u), 0, "e4m3").T @ mxq(dz, 0, "e5m2")
    dw1 = mxq(dz, 1, "e5m2") @ mxq(to_tokens(f64(x_norm)), 1, "e4m3").T
    return from_tokens(dx), dw1

@@ -1,0 +1,425 @@
+from contextlib import ExitStack
+
+import concourse.mybir as mybir
+from concourse.masks import make_identity
+
+F32 = mybir.dt.float32
+BF16 = mybir.dt.bfloat16
+U32 = mybir.dt.uint32
+U8 = mybir.dt.uint8
+E4 = mybir.dt.float8_e4m3fn_x4
+E5 = mybir.dt.float8_e5m2_x4
+ACT = mybir.ActivationFunctionType
+ALU = mybir.AluOpType
+
+P = 128
+FLOPS = 3 * 2 * 2048 * 512 * 512
+BYTES = (2 + 4 + 2 + 1 + 4 + 1) * 1024 * 1024
+EPS = 2.0 ** -31
+INV_SQRT_2PI = 0.3989422804014326779399460599343819
+
+
+def tile_getspatialgatingweights_pa_v_kernel(tc, x_norm, w1_u, b1_u, w2, b2, z, grad_out, out_0, out_1):
+    nc = tc.nc
+    z_v = z.rearrange("n (p t) d h w -> n p t (d h w)", t=4)
+    g_v = grad_out.rearrange("n (p t) d h w -> n p t (d h w)", t=4)
+    x_v = x_norm.rearrange("n (j p) d h w -> n p j (d h w)", p=P)
+    w1_v = w1_u.rearrange("(p j) c -> p j c", j=4)
+    w2_v = w2.rearrange("(p j) c -> p j c", j=4)
+    o0_v = out_0.rearrange("n c d h w -> n c (d h w)")
+    o1_v = out_1.rearrange("(p t) c -> p t c", t=4)
+
+    with ExitStack() as ctx:
+        keep = ctx.enter_context(tc.tile_pool(name="keep", bufs=1))
+        pool = ctx.enter_context(tc.tile_pool(name="pool", bufs=1))
+        ps = ctx.enter_context(tc.psum_pool(name="ps", bufs=1))
+
+        ident = keep.tile([P, P], F32, name="ident")
+        make_identity(nc, ident[:])
+        ident_k = keep.tile([P, P], F32, name="ident_k")
+        nc.vector.tensor_scalar(out=ident_k[:], in0=ident[:], scalar1=INV_SQRT_2PI, scalar2=None, op0=ALU.mult)
+        eps = keep.tile([P, 1], F32, name="eps")
+        nc.gpsimd.memset(eps[:], EPS)
+        warm = keep.tile([P, 1], F32, name="warm")
+        w2q = keep.tile([P, 1280], U32, name="w2q", align_bytes=64)
+        w2s = keep.tile([P, 1280], U8, name="w2s", align_bytes=64)
+        nc.gpsimd.memset(w2q[:], 0)
+        nc.gpsimd.memset(w2s[:].bitcast(U32), 0)
+        w1q = keep.tile([P, 512], U32, name="w1q", align_bytes=64)
+        w1s = keep.tile([P, 512], U8, name="w1s", align_bytes=64)
+
+        zt, gt, yt, lt = [None] * 4, [None] * 4, [None] * 4, [None] * 4
+        raw, deint = {}, {}
+        gq, xq, dq, oq = {}, {}, {}, {}
+        ks, dzb, dzi = {}, {}, {}
+        tr, du, po, sp = {}, {}, {}, {}
+        wraw, wi = {}, {}
+
+        def load_z(i, t0=0, t1=4):
+            n, hf = i // 2, i % 2
+            if zt[i] is None:
+                zt[i] = pool.tile([P, 2048], F32, name="zt", tag="zt", bufs=4)
+            nc.sync.dma_start(
+                out=zt[i][:, t0 * 512 : t1 * 512].rearrange("p (t x) -> p t x", t=t1 - t0),
+                in_=z_v[n, :, t0:t1, hf * 512 : (hf + 1) * 512])
+
+        def load_raw(key, view, n, t0=0, t1=4):
+            if key not in raw:
+                raw[key] = pool.tile([P, 4096], BF16, name="raw", tag="raw", bufs=2)
+            nc.sync.dma_start(out=raw[key][:, t0 * 1024 : t1 * 1024].rearrange("p (t x) -> p t x", t=t1 - t0), in_=view[n, :, t0:t1, :])
+
+        def load_w(key, view):
+            wraw[key] = pool.tile([P, 2048], BF16, name="wraw", tag="wraw", bufs=2)
+            nc.sync.dma_start(out=wraw[key][:].rearrange("p (j c) -> p j c", j=4), in_=view)
+
+        def w_inter(key):
+            wi[key] = pool.tile([P, 2048], BF16, name="wi", tag="wi", bufs=1, align_bytes=64)
+            nc.vector.tensor_copy(out=wi[key][:].rearrange("p (c j) -> p c j", j=4),
+                                  in_=wraw[key][:].rearrange("p (j c) -> p c j", j=4))
+
+        def w2_quant():
+            for hf in range(2):
+                lo = 256 + 512 * hf
+                nc.vector.quantize_mx(out=w2q[:, lo : lo + 256].bitcast(E4), scales=w2s[:, lo : lo + 256],
+                                      in_=wi["w2"][:, hf * 1024 : (hf + 1) * 1024])
+
+        def w1_quant():
+            nc.vector.quantize_mx(out=w1q[:].bitcast(E4), scales=w1s[:], in_=wi["w1"][:])
+
+        def separate(key, halves, t0=0, t1=4):
+            if key not in deint:
+                deint[key] = pool.tile([P, 4096], BF16, name="deint", tag="deint", bufs=2)
+            t, a = (t1 - t0) * halves, 64 // halves
+            words = slice(t0 * 512, t1 * 512)
+            nc.vector.tensor_copy(
+                out=deint[key][:].bitcast(F32)[:, words].rearrange("q (t p a w) -> q t p a w", t=t, p=2, a=a, w=4),
+                in_=raw[key][:].bitcast(F32)[:, words].rearrange("q (t a p w) -> q t p a w", t=t, p=2, a=a, w=4))
+
+        def transpose_bank(key, words, bases):
+            tr[key] = ps.tile([P, 2, 2, P], F32, name="tr", tag="tr", bufs=2)
+            for s, base in enumerate(bases):
+                for u in range(2):
+                    nc.tensor.transpose(tr[key][:, s, u, :], words[:, base + u : base + 256 : 2], ident[:])
+
+        def copy_bank(eng, key, dst, b):
+            words = dst[:].bitcast(F32)[:, b * 512 : (b + 1) * 512].rearrange("p (s c u) -> p s c u", s=2, u=2)
+            src = tr.pop(key)[:].rearrange("p s u c -> p s c u")
+            if eng == "v":
+                nc.vector.tensor_copy(out=words, in_=src)
+            else:
+                nc.scalar.copy(out=words, in_=src)
+
+        def new_ks(key):
+            ks[key] = pool.tile([P, 2048], BF16, name="ks", tag="ks", bufs=3, align_bytes=64)
+
+        def g_trans(n, p, b):
+            transpose_bank(("g", n, p, b), deint["g", n][:].bitcast(F32), [((2 * b + s) * 2 + p) * 256 for s in range(2)])
+
+        def x_trans(n, hf, b):
+            transpose_bank(("x", n, hf, b), deint["x", n][:].bitcast(F32), [((2 * b + s) * 2 + hf) * 256 for s in range(2)])
+
+        def d_trans(i, b):
+            transpose_bank(("d", i, b), dzb[i][:].bitcast(F32), [(2 * b + s) * 256 for s in range(2)])
+
+        def quant(store, key, name, src, fmt, bufs):
+            c = pool.tile([P, 512], U32, name=name + "c", tag=name + "c", bufs=bufs, align_bytes=64)
+            s = pool.tile([P, 512], U8, name=name + "s", tag=name + "s", bufs=bufs, align_bytes=64)
+            nc.vector.quantize_mx(out=c[:].bitcast(fmt), scales=s[:], in_=src[:])
+            store[key] = (c, s)
+
+        def stage_one(i, t):
+            n, hf = i // 2, i % 2
+            du[i, t] = ps.tile([P, 512], F32, name="mm", tag="mm", bufs=6)
+            for p in range(2):
+                lo = 512 * hf + (256 if p == 0 else 0)
+                c, s = gq[n, p]
+                nc.tensor.matmul_mx(out=du[i, t][:], lhsT=c[:, t * P : (t + 1) * P].bitcast(E5), lhsT_scale=s[:, t * P : (t + 1) * P],
+                                    rhs=w2q[:, lo : lo + 512].bitcast(E4), rhs_scale=w2s[:, lo : lo + 512],
+                                    start=(p == 0), stop=(p == 1))
+
+        def sq(i, a=0, b=2048):
+            if yt[i] is None:
+                yt[i] = pool.tile([P, 2048], F32, name="yt", tag="yt", bufs=3)
+            nc.scalar.activation(out=yt[i][:, a:b], in_=zt[i][:, a:b], func=ACT.Square, bias=eps[:])
+
+        def sq_shift(i):
+            yt[i] = pool.tile([P, 2048], F32, name="yt", tag="yt", bufs=3)
+            nc.vector.tensor_scalar(out=yt[i][:], in0=zt[i][:], scalar1=EPS, scalar2=None, op0=ALU.add)
+
+        def sq_square(i):
+            nc.vector.tensor_tensor(out=yt[i][:], in0=yt[i][:], in1=yt[i][:], op=ALU.mult)
+
+        def gelu(i, a=0, b=2048):
+            if gt[i] is None:
+                gt[i] = pool.tile([P, 2048], F32, name="gt", tag="gt", bufs=4)
+            nc.scalar.activation(out=gt[i][:, a:b], in_=zt[i][:, a:b], func=ACT.Gelu, bias=eps[:])
+
+        def ln(i):
+            lt[i] = pool.tile([P, 2048], F32, name="lt", tag="lt", bufs=2)
+            nc.scalar.activation(out=lt[i][:], in_=yt[i][:], func=ACT.Ln)
+
+        def recip(i):
+            nc.scalar.activation(out=lt[i][:], in_=lt[i][:], func=ACT.Exp, scale=-1.0)
+
+        def gauss(i):
+            nc.scalar.activation(out=yt[i][:], in_=yt[i][:], func=ACT.Exp, scale=-0.5)
+
+        def v_m(i, t0, t1):
+            cols = slice(t0 * 512, t1 * 512)
+            nc.vector.tensor_tensor(out=gt[i][:, cols], in0=gt[i][:, cols], in1=lt[i][:, cols], op=ALU.mult)
+
+        def v_s(i, t0, t1):
+            cols = slice(t0 * 512, t1 * 512)
+            nc.vector.scalar_tensor_tensor(out=gt[i][:, cols], in0=yt[i][:, cols], scalar=INV_SQRT_2PI, in1=gt[i][:, cols], op0=ALU.mult, op1=ALU.add)
+
+        def v_d(i, t0, t1):
+            cols = slice(t0 * 512, t1 * 512)
+            nc.vector.scalar_tensor_tensor(out=gt[i][:, cols], in0=zt[i][:, cols], scalar=EPS, in1=gt[i][:, cols], op0=ALU.add, op1=ALU.mult)
+
+        def pe_sum(i, t):
+            sp[i, t] = ps.tile([P, 512], F32, name="mm", tag="mm", bufs=6)
+            cols = slice(t * 512, (t + 1) * 512)
+            nc.tensor.matmul(out=sp[i, t][:], lhsT=ident[:], rhs=gt[i][:, cols], start=True, stop=False)
+            nc.tensor.matmul(out=sp[i, t][:], lhsT=ident_k[:], rhs=yt[i][:, cols], start=False, stop=True)
+
+        def v_dp(i, t):
+            cols = slice(t * 512, (t + 1) * 512)
+            nc.vector.scalar_tensor_tensor(out=gt[i][:, cols], in0=zt[i][:, cols], scalar=EPS, in1=sp.pop((i, t))[:], op0=ALU.add, op1=ALU.mult)
+
+        def v_dz(i, t):
+            if i not in dzb:
+                dzb[i] = pool.tile([P, 2048], BF16, name="dzb", tag="dzb", bufs=2)
+            nc.vector.tensor_tensor(
+                out=dzb[i][:, t * 512 : (t + 1) * 512].rearrange("q (p a w) -> q p a w", p=2, w=8),
+                in0=du.pop((i, t))[:].rearrange("q (p a w) -> q p a w", p=2, w=8),
+                in1=gt[i][:, t * 512 : (t + 1) * 512].rearrange("q (a p w) -> q p a w", p=2, w=8),
+                op=ALU.mult)
+
+        def inter(eng, i):
+            dzi[i] = pool.tile([P, 2048], BF16, name="dzi", tag="dzi", bufs=2, align_bytes=64)
+            dst = dzi[i][:].rearrange("p (c t) -> p c t", t=4)
+            src = dzb[i][:].rearrange("p (t c) -> p c t", t=4)
+            if eng == "v":
+                nc.vector.tensor_copy(out=dst, in_=src)
+            else:
+                nc.scalar.copy(out=dst, in_=src)
+
+        def mm_out0(i, cc, tag="mm"):
+            po[i, cc] = ps.tile([P, 512], F32, name="po", tag=tag, bufs=6 if tag == "mm" else 2)
+            c, s = oq[i]
+            nc.tensor.matmul_mx(out=po[i, cc][:], lhsT=w1q[:, cc * P : (cc + 1) * P].bitcast(E4), lhsT_scale=w1s[:, cc * P : (cc + 1) * P],
+                                rhs=c[:].bitcast(E5), rhs_scale=s[:], start=True, stop=True)
+
+        def out0(eng, i, cc):
+            n, hf = i // 2, i % 2
+            o = pool.tile([P, 512], F32, name="ost", tag="ost", bufs=6)
+            dst = o[:].rearrange("q (a p w) -> q p a w", p=2, w=8)
+            src = po.pop((i, cc))[:].rearrange("q (p a w) -> q p a w", p=2, w=8)
+            if eng == "v":
+                nc.vector.tensor_copy(out=dst, in_=src)
+            else:
+                nc.scalar.copy(out=dst, in_=src)
+            nc.sync.dma_start(out=o0_v[n, cc * P : (cc + 1) * P, hf * 512 : (hf + 1) * 512], in_=o[:])
+
+        o1, o1s = {}, {}
+
+        def mm_out1(t, i):
+            if t not in o1:
+                o1[t] = ps.tile([P, 512], F32, name="mm", tag="mm", bufs=6)
+            dc, ds = dq[i]
+            xc, xs = xq[i]
+            nc.tensor.matmul_mx(out=o1[t][:], lhsT=dc[:, t * P : (t + 1) * P].bitcast(E5), lhsT_scale=ds[:, t * P : (t + 1) * P],
+                                rhs=xc[:].bitcast(E4), rhs_scale=xs[:], start=(i == 0), stop=(i == 3))
+
+        def out1(eng, t):
+            if t % 2 == 0:
+                o1s[t // 2] = pool.tile([P, 1024], F32, name="o1s", tag="raw", bufs=2)
+            o = o1s[t // 2][:, (t % 2) * 512 : (t % 2) * 512 + 512]
+            if eng == "v":
+                nc.vector.tensor_copy(out=o, in_=o1[t][:])
+            else:
+                nc.scalar.copy(out=o, in_=o1[t][:])
+            nc.sync.dma_start(out=o1_v[:, t, :], in_=o)
+
+        def g_path(n, p, b):
+            if b == 0:
+                new_ks(("g", n, p))
+            g_trans(n, p, b)
+            copy_bank("v", ("g", n, p, b), ks["g", n, p], b)
+
+        def x_part(eng, i):
+            n, hf = i // 2, i % 2
+            new_ks(("x", i))
+            for b in range(2):
+                x_trans(n, hf, b)
+                copy_bank(eng, ("x", n, hf, b), ks["x", i], b)
+
+        def dt_part(eng, i):
+            new_ks(("d", i))
+            for b in (1, 0):
+                d_trans(i, b)
+                copy_bank(eng, ("d", i, b), ks["d", i], b)
+
+        def ew_first(i):
+            v_m(i, 0, 2)
+            v_m(i, 2, 4)
+            for t in range(2):
+                pe_sum(i, t)
+            v_s(i, 2, 4)
+
+        def ew_second(i):
+            v_d(i, 2, 4)
+            for t in (2, 3):
+                v_dz(i, t)
+
+        def ew_third(i):
+            for t in range(2):
+                v_dp(i, t)
+            for t in range(2):
+                v_dz(i, t)
+
+        def all_stage_one(i):
+            for t in (2, 3, 0, 1):
+                stage_one(i, t)
+
+        def all_mm_out0(i):
+            for cc in range(4):
+                mm_out0(i, cc)
+
+        def all_out0(eng, i):
+            for cc in range(4):
+                out0(eng, i, cc)
+
+        def q_g(n, p):
+            quant(gq, (n, p), "gq", ks["g", n, p], E5, 4)
+
+        def q_x(i):
+            quant(xq, i, "xq", ks["x", i], E4, 4)
+
+        def q_o(i):
+            quant(oq, i, "oq", dzi[i], E5, 2)
+
+        def q_d(i):
+            quant(dq, i, "dq", ks["d", i], E5, 4)
+
+        with tc.manual_schedule():
+            load_z(0, 0, 2)
+            load_raw(("g", 0), g_v, 0, 0, 2)
+            load_z(0, 2, 4)
+            load_raw(("g", 0), g_v, 0, 2, 4)
+            load_z(1)
+            load_w("w2", w2_v)
+            load_w("w1", w1_v)
+            load_z(2)
+            load_z(3)
+            load_raw(("g", 1), g_v, 1)
+            nc.scalar.activation(out=warm[:], in_=eps[:], func=ACT.Gelu)
+            for h in range(2):
+                sq(0, h * 1024, h * 1024 + 1024)
+                gelu(0, h * 1024, h * 1024 + 1024)
+            sq(1)
+            gelu(1)
+            gelu(2)
+            gelu(3)
+            ln(0)
+            ln(1)
+            recip(0)
+            gauss(0)
+            recip(1)
+            gauss(1)
+            separate(("g", 0), 1, 0, 2)
+            g_path(0, 0, 0)
+            g_path(0, 1, 0)
+            separate(("g", 0), 1, 2, 4)
+            g_path(0, 0, 1)
+            g_path(0, 1, 1)
+            w_inter("w2")
+            load_raw(("x", 0), x_v, 0)
+            q_g(0, 0)
+            w2_quant()
+            q_g(0, 1)
+            w_inter("w1")
+            sq_shift(2)
+            w1_quant()
+            sq_square(2)
+            separate(("g", 1), 1)
+            load_raw(("x", 1), x_v, 1)
+            g_path(1, 0, 0)
+            g_path(1, 0, 1)
+            g_path(1, 1, 0)
+            g_path(1, 1, 1)
+            all_stage_one(0)
+            separate(("x", 0), 2)
+            q_g(1, 0)
+            q_g(1, 1)
+            x_part("v", 0)
+            q_x(0)
+
+            sq(3)
+            ln(2)
+            ln(3)
+            recip(2)
+            gauss(2)
+
+            ew_first(0)
+            ew_second(0)
+            ew_third(0)
+            all_stage_one(1)
+            dt_part("s", 0)
+            ew_first(1)
+            inter("v", 0)
+            ew_second(1)
+            q_o(0)
+            all_mm_out0(0)
+            all_out0("s", 0)
+            ew_third(1)
+            recip(3)
+            all_stage_one(2)
+            dt_part("s", 1)
+            gauss(3)
+            ew_first(2)
+            inter("v", 1)
+            ew_second(2)
+            q_o(1)
+            q_d(0)
+            q_d(1)
+            all_mm_out0(1)
+            all_out0("s", 1)
+            ew_third(2)
+            all_stage_one(3)
+            dt_part("s", 2)
+            inter("s", 2)
+            separate(("x", 1), 2)
+            x_part("s", 1)
+            ew_first(3)
+            q_d(2)
+            ew_second(3)
+            q_x(1)
+            q_o(2)
+            x_part("s", 2)
+            all_mm_out0(2)
+            all_out0("s", 2)
+            ew_third(3)
+            x_part("s", 3)
+            q_x(2)
+            dt_part("s", 3)
+            inter("v", 3)
+            for t in range(2):
+                for i in range(3):
+                    mm_out1(t, i)
+            q_o(3)
+            q_x(3)
+            q_d(3)
+            mm_out0(3, 0)
+            mm_out0(3, 1)
+            mm_out0(3, 2, "tr")
+            mm_out0(3, 3, "tr")
+            for cc in range(4):
+                out0("s" if cc % 2 == 0 else "v", 3, cc)
+            for t in range(2, 4):
+                for i in range(3):
+                    mm_out1(t, i)
+            for t in range(4):
+                mm_out1(t, 3)
+            for t in range(4):
+                out1("s" if t % 2 == 0 else "v", t)

@@ -36,8 +36,9 @@ def tile_getspatialgatingweights_pa_v_kernel(tc, x_norm, w1_u, b1_u, w2, b2, z, 
 
         ident = keep.tile([P, P], F32, name="ident")
         make_identity(nc, ident[:])
-        ident_k = keep.tile([P, P], F32, name="ident_k")
-        nc.vector.tensor_scalar(out=ident_k[:], in0=ident[:], scalar1=INV_SQRT_2PI, scalar2=None, op0=ALU.mult)
+        ones = keep.tile([P, 1], F32, name="ones")
+        nc.gpsimd.memset(ones[:], 1.0)
+        lnk = keep.tile([P, 1], F32, name="lnk")
         eps = keep.tile([P, 1], F32, name="eps")
         nc.gpsimd.memset(eps[:], EPS)
         warm = keep.tile([P, 1], F32, name="warm")
@@ -52,8 +53,8 @@ def tile_getspatialgatingweights_pa_v_kernel(tc, x_norm, w1_u, b1_u, w2, b2, z, 
         raw, deint = {}, {}
         gq, xq, dq, oq = {}, {}, {}, {}
         ks, dzb, dzi = {}, {}, {}
-        tr, du, po, sp = {}, {}, {}, {}
-        wraw, wi = {}, {}
+        tr, du, po, sp, zp, hb = {}, {}, {}, {}, {}, {}
+        wraw, wi, ost = {}, {}, {}
 
         def load_z(i, t0=0, t1=4):
             n, hf = i // 2, i % 2
@@ -109,13 +110,14 @@ def tile_getspatialgatingweights_pa_v_kernel(tc, x_norm, w1_u, b1_u, w2, b2, z, 
             else:
                 nc.scalar.copy(out=words, in_=src)
 
-        def new_ks(key):
-            ks[key] = pool.tile([P, 2048], BF16, name="ks", tag="ks", bufs=3, align_bytes=64)
+        def new_ks(key, eng):
+            ks[key] = pool.tile([P, 2048], BF16, name="k" + eng, tag="k" + eng, bufs=2, align_bytes=64)
 
         def g_trans(n, p, b):
             transpose_bank(("g", n, p, b), deint["g", n][:].bitcast(F32), [((2 * b + s) * 2 + p) * 256 for s in range(2)])
 
-        def x_trans(n, hf, b):
+        def x_trans(i, b):
+            n, hf = i // 2, i % 2
             transpose_bank(("x", n, hf, b), deint["x", n][:].bitcast(F32), [((2 * b + s) * 2 + hf) * 256 for s in range(2)])
 
         def d_trans(i, b):
@@ -129,7 +131,7 @@ def tile_getspatialgatingweights_pa_v_kernel(tc, x_norm, w1_u, b1_u, w2, b2, z, 
 
         def stage_one(i, t):
             n, hf = i // 2, i % 2
-            du[i, t] = ps.tile([P, 512], F32, name="mm", tag="mm", bufs=6)
+            du[i, t] = ps.tile([P, 512], F32, name="mm", tag="mm", bufs=4)
             for p in range(2):
                 lo = 512 * hf + (256 if p == 0 else 0)
                 c, s = gq[n, p]
@@ -137,54 +139,45 @@ def tile_getspatialgatingweights_pa_v_kernel(tc, x_norm, w1_u, b1_u, w2, b2, z, 
                                     rhs=w2q[:, lo : lo + 512].bitcast(E4), rhs_scale=w2s[:, lo : lo + 512],
                                     start=(p == 0), stop=(p == 1))
 
-        def sq(i, a=0, b=2048):
-            if yt[i] is None:
-                yt[i] = pool.tile([P, 2048], F32, name="yt", tag="yt", bufs=3)
-            nc.scalar.activation(out=yt[i][:, a:b], in_=zt[i][:, a:b], func=ACT.Square, bias=eps[:])
-
-        def sq_shift(i):
-            yt[i] = pool.tile([P, 2048], F32, name="yt", tag="yt", bufs=3)
-            nc.vector.tensor_scalar(out=yt[i][:], in0=zt[i][:], scalar1=EPS, scalar2=None, op0=ALU.add)
-
-        def sq_square(i):
-            nc.vector.tensor_tensor(out=yt[i][:], in0=yt[i][:], in1=yt[i][:], op=ALU.mult)
-
-        def gelu(i, a=0, b=2048):
-            if gt[i] is None:
-                gt[i] = pool.tile([P, 2048], F32, name="gt", tag="gt", bufs=4)
-            nc.scalar.activation(out=gt[i][:, a:b], in_=zt[i][:, a:b], func=ACT.Gelu, bias=eps[:])
-
         def ln(i):
-            lt[i] = pool.tile([P, 2048], F32, name="lt", tag="lt", bufs=2)
+            lt[i] = pool.tile([P, 2048], F32, name="lt", tag="lt", bufs=3)
             nc.scalar.activation(out=lt[i][:], in_=yt[i][:], func=ACT.Ln)
 
         def recip(i):
             nc.scalar.activation(out=lt[i][:], in_=lt[i][:], func=ACT.Exp, scale=-1.0)
 
+        def v_m(eng, i, t0, t1):
+            cols = slice(t0 * 512, t1 * 512)
+            (nc.vector if eng == "v" else nc.gpsimd).tensor_tensor(out=gt[i][:, cols], in0=gt[i][:, cols], in1=lt[i][:, cols], op=ALU.mult)
+
+        def z_trans(i, t):
+            zp[i, t] = ps.tile([P, 4, P], F32, name="po", tag="po", bufs=2)
+            for b in range(4):
+                nc.tensor.transpose(zp[i, t][:, b, :], zt[i][:, t * 512 + b * P : t * 512 + b * P + P], ident[:])
+
+        def sq(i, t):
+            if yt[i] is None:
+                yt[i] = pool.tile([P, 2048], F32, name="yt", tag="yt", bufs=3)
+            nc.scalar.activation(out=yt[i][:, t * 512 : (t + 1) * 512], in_=zp[i, t][:].rearrange("q b c -> q (b c)"), func=ACT.Square, bias=eps[:])
+
+        def gelu(i, t):
+            if gt[i] is None:
+                gt[i] = pool.tile([P, 2048], F32, name="gt", tag="gt", bufs=3)
+            nc.scalar.activation(out=gt[i][:, t * 512 : (t + 1) * 512], in_=zp[i, t][:].rearrange("q b c -> q (b c)"), func=ACT.Gelu, bias=eps[:])
+
         def gauss(i):
-            nc.scalar.activation(out=yt[i][:], in_=yt[i][:], func=ACT.Exp, scale=-0.5)
-
-        def v_m(i, t0, t1):
-            cols = slice(t0 * 512, t1 * 512)
-            nc.vector.tensor_tensor(out=gt[i][:, cols], in0=gt[i][:, cols], in1=lt[i][:, cols], op=ALU.mult)
-
-        def v_s(i, t0, t1):
-            cols = slice(t0 * 512, t1 * 512)
-            nc.vector.scalar_tensor_tensor(out=gt[i][:, cols], in0=yt[i][:, cols], scalar=INV_SQRT_2PI, in1=gt[i][:, cols], op0=ALU.mult, op1=ALU.add)
-
-        def v_d(i, t0, t1):
-            cols = slice(t0 * 512, t1 * 512)
-            nc.vector.scalar_tensor_tensor(out=gt[i][:, cols], in0=zt[i][:, cols], scalar=EPS, in1=gt[i][:, cols], op0=ALU.add, op1=ALU.mult)
+            nc.scalar.activation(out=yt[i][:], in_=yt[i][:], func=ACT.Exp, scale=-0.5, bias=lnk[:])
 
         def pe_sum(i, t):
-            sp[i, t] = ps.tile([P, 512], F32, name="mm", tag="mm", bufs=6)
-            cols = slice(t * 512, (t + 1) * 512)
-            nc.tensor.matmul(out=sp[i, t][:], lhsT=ident[:], rhs=gt[i][:, cols], start=True, stop=False)
-            nc.tensor.matmul(out=sp[i, t][:], lhsT=ident_k[:], rhs=yt[i][:, cols], start=False, stop=True)
+            sp[i, t] = ps.tile([P, 512], F32, name="mm", tag="mm", bufs=4)
+            for k, src in enumerate((gt[i], yt[i])):
+                for b in range(4):
+                    nc.tensor.matmul(out=sp[i, t][:, b * P : b * P + P], lhsT=src[:, t * 512 + b * P : t * 512 + b * P + P], rhs=ident[:],
+                                     is_transpose=(k == 1 or b >= 2), start=(k == 0 and b == 0), stop=(k == 1 and b == 3))
 
         def v_dp(i, t):
             cols = slice(t * 512, (t + 1) * 512)
-            nc.vector.scalar_tensor_tensor(out=gt[i][:, cols], in0=zt[i][:, cols], scalar=EPS, in1=sp.pop((i, t))[:], op0=ALU.add, op1=ALU.mult)
+            nc.vector.scalar_tensor_tensor(out=zt[i][:, cols], in0=zt[i][:, cols], scalar=EPS, in1=sp.pop((i, t))[:], op0=ALU.add, op1=ALU.mult)
 
         def v_dz(i, t):
             if i not in dzb:
@@ -192,11 +185,11 @@ def tile_getspatialgatingweights_pa_v_kernel(tc, x_norm, w1_u, b1_u, w2, b2, z, 
             nc.vector.tensor_tensor(
                 out=dzb[i][:, t * 512 : (t + 1) * 512].rearrange("q (p a w) -> q p a w", p=2, w=8),
                 in0=du.pop((i, t))[:].rearrange("q (p a w) -> q p a w", p=2, w=8),
-                in1=gt[i][:, t * 512 : (t + 1) * 512].rearrange("q (a p w) -> q p a w", p=2, w=8),
+                in1=zt[i][:, t * 512 : (t + 1) * 512].rearrange("q (a p w) -> q p a w", p=2, w=8),
                 op=ALU.mult)
 
         def inter(eng, i):
-            dzi[i] = pool.tile([P, 2048], BF16, name="dzi", tag="dzi", bufs=2, align_bytes=64)
+            dzi[i] = pool.tile([P, 2048], BF16, name="dzi", tag="dzi" + eng, bufs=1, align_bytes=64)
             dst = dzi[i][:].rearrange("p (c t) -> p c t", t=4)
             src = dzb[i][:].rearrange("p (t c) -> p c t", t=4)
             if eng == "v":
@@ -204,91 +197,62 @@ def tile_getspatialgatingweights_pa_v_kernel(tc, x_norm, w1_u, b1_u, w2, b2, z, 
             else:
                 nc.scalar.copy(out=dst, in_=src)
 
-        def mm_out0(i, cc, tag="mm"):
-            po[i, cc] = ps.tile([P, 512], F32, name="po", tag=tag, bufs=6 if tag == "mm" else 2)
+        def mm_out0(i, cc, tag="po"):
+            po[i, cc] = ps.tile([P, 512], F32, name="po", tag=tag, bufs=2)
             c, s = oq[i]
             nc.tensor.matmul_mx(out=po[i, cc][:], lhsT=w1q[:, cc * P : (cc + 1) * P].bitcast(E4), lhsT_scale=w1s[:, cc * P : (cc + 1) * P],
                                 rhs=c[:].bitcast(E5), rhs_scale=s[:], start=True, stop=True)
 
         def out0(eng, i, cc):
-            n, hf = i // 2, i % 2
-            o = pool.tile([P, 512], F32, name="ost", tag="ost", bufs=6)
+            o = pool.tile([P, 512], F32, name="ost", tag="ost" + eng, bufs=3)
             dst = o[:].rearrange("q (a p w) -> q p a w", p=2, w=8)
             src = po.pop((i, cc))[:].rearrange("q (p a w) -> q p a w", p=2, w=8)
             if eng == "v":
                 nc.vector.tensor_copy(out=dst, in_=src)
             else:
                 nc.scalar.copy(out=dst, in_=src)
-            nc.sync.dma_start(out=o0_v[n, cc * P : (cc + 1) * P, hf * 512 : (hf + 1) * 512], in_=o[:])
+            ost[i, cc] = o
+
+        def st0(i, cc):
+            n, hf = i // 2, i % 2
+            nc.sync.dma_start(out=o0_v[n, cc * P : (cc + 1) * P, hf * 512 : (hf + 1) * 512], in_=ost.pop((i, cc))[:])
 
         o1, o1s = {}, {}
 
         def mm_out1(t, i):
             if t not in o1:
-                o1[t] = ps.tile([P, 512], F32, name="mm", tag="mm", bufs=6)
+                o1[t] = ps.tile([P, 512], F32, name="mm", tag="mm", bufs=4)
             dc, ds = dq[i]
             xc, xs = xq[i]
             nc.tensor.matmul_mx(out=o1[t][:], lhsT=dc[:, t * P : (t + 1) * P].bitcast(E5), lhsT_scale=ds[:, t * P : (t + 1) * P],
                                 rhs=xc[:].bitcast(E4), rhs_scale=xs[:], start=(i == 0), stop=(i == 3))
 
         def out1(eng, t):
-            if t % 2 == 0:
+            if t // 2 not in o1s:
                 o1s[t // 2] = pool.tile([P, 1024], F32, name="o1s", tag="raw", bufs=2)
             o = o1s[t // 2][:, (t % 2) * 512 : (t % 2) * 512 + 512]
             if eng == "v":
                 nc.vector.tensor_copy(out=o, in_=o1[t][:])
             else:
                 nc.scalar.copy(out=o, in_=o1[t][:])
-            nc.sync.dma_start(out=o1_v[:, t, :], in_=o)
 
-        def g_path(n, p, b):
-            if b == 0:
-                new_ks(("g", n, p))
-            g_trans(n, p, b)
-            copy_bank("v", ("g", n, p, b), ks["g", n, p], b)
+        def st1(t):
+            nc.sync.dma_start(out=o1_v[:, t, :], in_=o1s[t // 2][:, (t % 2) * 512 : (t % 2) * 512 + 512])
 
-        def x_part(eng, i):
-            n, hf = i // 2, i % 2
-            new_ks(("x", i))
+        def g_copy(eng, n, p, b):
+            if ("g", n, p) not in ks:
+                new_ks(("g", n, p), eng)
+            copy_bank(eng, ("g", n, p, b), ks["g", n, p], b)
+
+        def x_copy(eng, i):
+            new_ks(("x", i), eng)
             for b in range(2):
-                x_trans(n, hf, b)
-                copy_bank(eng, ("x", n, hf, b), ks["x", i], b)
+                copy_bank(eng, ("x", i // 2, i % 2, b), ks["x", i], b)
 
-        def dt_part(eng, i):
-            new_ks(("d", i))
-            for b in (1, 0):
-                d_trans(i, b)
+        def d_copy(eng, i):
+            new_ks(("d", i), eng)
+            for b in range(2):
                 copy_bank(eng, ("d", i, b), ks["d", i], b)
-
-        def ew_first(i):
-            v_m(i, 0, 2)
-            v_m(i, 2, 4)
-            for t in range(2):
-                pe_sum(i, t)
-            v_s(i, 2, 4)
-
-        def ew_second(i):
-            v_d(i, 2, 4)
-            for t in (2, 3):
-                v_dz(i, t)
-
-        def ew_third(i):
-            for t in range(2):
-                v_dp(i, t)
-            for t in range(2):
-                v_dz(i, t)
-
-        def all_stage_one(i):
-            for t in (2, 3, 0, 1):
-                stage_one(i, t)
-
-        def all_mm_out0(i):
-            for cc in range(4):
-                mm_out0(i, cc)
-
-        def all_out0(eng, i):
-            for cc in range(4):
-                out0(eng, i, cc)
 
         def q_g(n, p):
             quant(gq, (n, p), "gq", ks["g", n, p], E5, 4)
@@ -302,124 +266,327 @@ def tile_getspatialgatingweights_pa_v_kernel(tc, x_norm, w1_u, b1_u, w2, b2, z, 
         def q_d(i):
             quant(dq, i, "dq", ks["d", i], E5, 4)
 
-        with tc.manual_schedule():
-            load_z(0, 0, 2)
-            load_raw(("g", 0), g_v, 0, 0, 2)
-            load_z(0, 2, 4)
-            load_raw(("g", 0), g_v, 0, 2, 4)
-            load_z(1)
+        def sep_g(n, t0, t1):
+            separate(("g", n), 1, t0, t1)
+
+        def sep_x(n):
+            separate(("x", n), 2)
+
+        def ld_g(n, t0, t1):
+            load_raw(("g", n), g_v, n, t0, t1)
+
+        def ld_x(n):
+            load_raw(("x", n), x_v, n)
+
+        def ld_w2():
             load_w("w2", w2_v)
+
+        def ld_w1():
             load_w("w1", w1_v)
-            load_z(2)
-            load_z(3)
-            load_raw(("g", 1), g_v, 1)
+
+        def heat():
+            if "t" not in hb:
+                hb["t"] = ps.tile([P, 256], F32, name="mm", tag="mm", bufs=4)
+            nc.tensor.matmul(out=hb["t"][:], lhsT=ident[:], rhs=zt[0][:, :256], start=True, stop=True)
+
+        def warmup():
+            nc.scalar.activation(out=lnk[:], in_=ones[:], func=ACT.Ln, scale=INV_SQRT_2PI)
             nc.scalar.activation(out=warm[:], in_=eps[:], func=ACT.Gelu)
-            for h in range(2):
-                sq(0, h * 1024, h * 1024 + 1024)
-                gelu(0, h * 1024, h * 1024 + 1024)
-            sq(1)
-            gelu(1)
-            gelu(2)
-            gelu(3)
+
+        with tc.manual_schedule():
+            load_z(0, 2, 4)
+            z_trans(0, 2)
+            load_z(0, 0, 2)
+            ld_g(0, 2, 4)
+            z_trans(0, 3)
+            heat()
+            load_z(1)
+            ld_g(0, 0, 2)
+            warmup()
+            z_trans(0, 0)
+            heat()
+            z_trans(0, 1)
+            sq(0, 2)
+            gelu(0, 2)
+            ld_w2()
+            heat()
+            z_trans(1, 2)
+            z_trans(1, 0)
+            sq(0, 3)
+            w_inter("w2")
+            heat()
+            ld_g(1, 0, 4)
+            sep_g(0, 0, 2)
+            load_z(2)
+            z_trans(1, 1)
+            sep_g(0, 2, 4)
+            gelu(0, 3)
+            z_trans(1, 3)
+            gelu(0, 0)
+            g_trans(0, 1, 0)
+            heat()
+            g_trans(0, 0, 0)
+            sep_g(1, 0, 4)
+            ld_x(0)
+            g_copy("v", 0, 1, 0)
+            g_trans(0, 0, 1)
+            g_copy("v", 0, 0, 1)
+            heat()
+            sq(0, 0)
+            gelu(0, 1)
+            sq(0, 1)
+            gelu(1, 2)
+            ld_w1()
+            g_trans(0, 1, 1)
+            heat()
+            g_copy("v", 0, 1, 1)
+            heat()
+            gelu(1, 0)
+            sq(1, 0)
+            sq(1, 2)
+            g_trans(1, 1, 1)
+            g_trans(1, 1, 0)
+            q_g(0, 1)
+            sq(1, 1)
+            sep_x(0)
+            z_trans(2, 0)
+            w2_quant()
+            g_copy("v", 0, 0, 0)
+            sq(1, 3)
+            x_trans(0, 0)
+            gelu(1, 1)
+            z_trans(2, 2)
+            gelu(1, 3)
             ln(0)
+            g_copy("v", 1, 1, 1)
             ln(1)
             recip(0)
-            gauss(0)
-            recip(1)
-            gauss(1)
-            separate(("g", 0), 1, 0, 2)
-            g_path(0, 0, 0)
-            g_path(0, 1, 0)
-            separate(("g", 0), 1, 2, 4)
-            g_path(0, 0, 1)
-            g_path(0, 1, 1)
-            w_inter("w2")
-            load_raw(("x", 0), x_v, 0)
-            q_g(0, 0)
-            w2_quant()
-            q_g(0, 1)
             w_inter("w1")
-            sq_shift(2)
-            w1_quant()
-            sq_square(2)
-            separate(("g", 1), 1)
-            load_raw(("x", 1), x_v, 1)
-            g_path(1, 0, 0)
-            g_path(1, 0, 1)
-            g_path(1, 1, 0)
-            g_path(1, 1, 1)
-            all_stage_one(0)
-            separate(("x", 0), 2)
-            q_g(1, 0)
+            q_g(0, 0)
+            heat()
+            g_copy("v", 1, 1, 0)
+            x_trans(0, 1)
+            v_m("v", 0, 0, 2)
+            v_m("v", 0, 2, 4)
+            heat()
+            load_z(3)
+            recip(1)
+            gauss(0)
+            gauss(1)
+            pe_sum(0, 1)
+            pe_sum(0, 3)
+            g_trans(1, 0, 0)
+            v_m("v", 1, 2, 4)
+            pe_sum(0, 2)
+            g_trans(1, 0, 1)
+            stage_one(1, 2)
+            pe_sum(1, 2)
+            x_copy("v", 0)
+            v_dp(0, 1)
+            z_trans(2, 1)
+            sq(2, 0)
+            stage_one(0, 3)
             q_g(1, 1)
-            x_part("v", 0)
+            w1_quant()
+            z_trans(2, 3)
+            v_dp(0, 2)
+            v_m("v", 1, 0, 2)
+            pe_sum(0, 0)
+            v_dp(0, 3)
+            gelu(2, 0)
+            z_trans(3, 2)
+            g_copy("v", 1, 0, 0)
+            stage_one(0, 1)
+            sq(2, 2)
+            stage_one(0, 0)
+            z_trans(3, 0)
+            ld_x(1)
+            stage_one(0, 2)
+            gelu(2, 2)
+            v_dp(1, 2)
             q_x(0)
-
-            sq(3)
+            v_dz(1, 2)
+            v_dp(0, 0)
+            sq(2, 1)
+            g_copy("v", 1, 0, 1)
+            v_dz(0, 3)
+            z_trans(3, 3)
+            v_dz(0, 0)
+            v_dz(0, 1)
+            z_trans(3, 1)
+            v_dz(0, 2)
+            pe_sum(1, 3)
+            gelu(2, 1)
+            sq(2, 3)
+            gelu(2, 3)
+            sq(3, 2)
+            d_trans(0, 0)
+            q_g(1, 0)
+            pe_sum(1, 1)
+            gelu(3, 2)
+            d_trans(0, 1)
+            gelu(3, 0)
+            stage_one(1, 3)
+            stage_one(1, 0)
+            pe_sum(1, 0)
+            inter("v", 0)
+            sq(3, 0)
+            v_dp(1, 3)
+            gelu(3, 3)
+            q_o(0)
+            x_trans(1, 1)
+            gelu(3, 1)
+            sq(3, 3)
+            d_copy("v", 0)
+            v_dp(1, 1)
+            stage_one(1, 1)
+            sep_x(1)
+            sq(3, 1)
             ln(2)
+            x_trans(1, 0)
+            q_d(0)
+            x_trans(2, 0)
+            v_dp(1, 0)
+            x_copy("v", 1)
+            v_dz(1, 1)
+            v_dz(1, 3)
+            v_dz(1, 0)
+            x_trans(2, 1)
             ln(3)
+            mm_out0(0, 0)
+            mm_out0(0, 1)
             recip(2)
             gauss(2)
-
-            ew_first(0)
-            ew_second(0)
-            ew_third(0)
-            all_stage_one(1)
-            dt_part("s", 0)
-            ew_first(1)
-            inter("v", 0)
-            ew_second(1)
-            q_o(0)
-            all_mm_out0(0)
-            all_out0("s", 0)
-            ew_third(1)
-            recip(3)
-            all_stage_one(2)
-            dt_part("s", 1)
-            gauss(3)
-            ew_first(2)
-            inter("v", 1)
-            ew_second(2)
-            q_o(1)
-            q_d(0)
-            q_d(1)
-            all_mm_out0(1)
-            all_out0("s", 1)
-            ew_third(2)
-            all_stage_one(3)
-            dt_part("s", 2)
-            inter("s", 2)
-            separate(("x", 1), 2)
-            x_part("s", 1)
-            ew_first(3)
-            q_d(2)
-            ew_second(3)
+            out0("s", 0, 0)
+            stage_one(2, 0)
             q_x(1)
-            q_o(2)
-            x_part("s", 2)
-            all_mm_out0(2)
-            all_out0("s", 2)
-            ew_third(3)
-            x_part("s", 3)
+            v_m("v", 2, 0, 2)
+            v_m("v", 2, 2, 4)
+            stage_one(2, 3)
+            pe_sum(2, 0)
+            pe_sum(2, 3)
+            inter("v", 1)
+            mm_out0(0, 2)
+            d_trans(1, 0)
+            pe_sum(2, 1)
+            pe_sum(2, 2)
+            v_dp(2, 0)
+            d_trans(1, 1)
+            x_copy("s", 2)
+            out0("s", 0, 1)
+            recip(3)
+            v_dp(2, 3)
+            out0("s", 0, 2)
+            v_dz(2, 0)
+            stage_one(2, 1)
+            q_o(1)
+            gauss(3)
+            d_copy("s", 1)
+            mm_out0(0, 3)
+            v_dp(2, 1)
+            st0(0, 0)
+            v_dz(2, 3)
+            stage_one(2, 2)
+            v_m("v", 3, 2, 4)
+            v_dz(2, 1)
+            v_dp(2, 2)
+            v_m("v", 3, 0, 2)
+            mm_out0(1, 1)
+            pe_sum(3, 3)
+            v_dz(2, 2)
+            pe_sum(3, 2)
+            q_d(1)
+            d_trans(2, 0)
             q_x(2)
-            dt_part("s", 3)
+            pe_sum(3, 1)
+            pe_sum(3, 0)
+            d_trans(2, 1)
+            st0(0, 1)
+            mm_out0(1, 0)
+            out0("s", 0, 3)
+            inter("s", 2)
+            stage_one(3, 2)
+            mm_out0(1, 2)
+            st0(0, 2)
+            out0("s", 1, 1)
+            out0("s", 1, 0)
+            stage_one(3, 3)
+            v_dp(3, 3)
+            v_dp(3, 1)
+            v_dp(3, 2)
+            q_o(2)
+            st0(0, 3)
+            d_copy("s", 2)
+            out0("v", 1, 2)
+            mm_out0(2, 2)
+            stage_one(3, 1)
+            st0(1, 1)
+            v_dp(3, 0)
+            x_trans(3, 0)
+            x_trans(3, 1)
+            v_dz(3, 3)
+            stage_one(3, 0)
+            mm_out0(2, 0)
+            mm_out1(1, 0)
+            out0("s", 2, 2)
+            st0(1, 0)
+            mm_out0(2, 3)
+            x_copy("s", 3)
+            mm_out1(1, 1)
+            v_dz(3, 2)
+            st0(2, 2)
+            mm_out0(1, 3)
+            d_trans(3, 1)
+            out0("s", 2, 0)
+            v_dz(3, 1)
+            v_dz(3, 0)
+            out0("s", 2, 3)
+            out0("s", 1, 3)
+            q_d(2)
             inter("v", 3)
-            for t in range(2):
-                for i in range(3):
-                    mm_out1(t, i)
             q_o(3)
-            q_x(3)
-            q_d(3)
+            d_trans(3, 0)
+            mm_out1(1, 2)
+            mm_out1(0, 0)
+            st0(2, 0)
+            mm_out0(2, 1)
             mm_out0(3, 0)
-            mm_out0(3, 1)
-            mm_out0(3, 2, "tr")
             mm_out0(3, 3, "tr")
-            for cc in range(4):
-                out0("s" if cc % 2 == 0 else "v", 3, cc)
-            for t in range(2, 4):
-                for i in range(3):
-                    mm_out1(t, i)
-            for t in range(4):
-                mm_out1(t, 3)
-            for t in range(4):
-                out1("s" if t % 2 == 0 else "v", t)
+            out0("v", 2, 1)
+            st0(2, 3)
+            mm_out1(3, 0)
+            mm_out0(3, 1)
+            d_copy("s", 3)
+            q_d(3)
+            out0("s", 3, 0)
+            mm_out0(3, 2, "tr")
+            q_x(3)
+            mm_out1(0, 1)
+            mm_out1(3, 1)
+            st0(1, 3)
+            st0(1, 2)
+            out0("v", 3, 2)
+            mm_out1(3, 2)
+            mm_out1(3, 3)
+            out0("s", 3, 3)
+            out0("s", 3, 1)
+            out1("s", 3)
+            mm_out1(0, 2)
+            st0(2, 1)
+            st0(3, 0)
+            mm_out1(1, 3)
+            st0(3, 3)
+            mm_out1(0, 3)
+            st0(3, 1)
+            st0(3, 2)
+            mm_out1(2, 0)
+            out1("s", 1)
+            mm_out1(2, 1)
+            out1("s", 0)
+            mm_out1(2, 2)
+            mm_out1(2, 3)
+            out1("v", 2)
+            st1(3)
+            st1(1)
+            st1(0)
+            st1(2)

@@ -160,6 +160,15 @@ def tile_getspatialgatingweights_pa_v_kernel(tc, x_norm, w1_u, b1_u, w2, b2, z, 
                 yt[i] = pool.tile([P, 2048], F32, name="yt", tag="yt", bufs=3)
             nc.scalar.activation(out=yt[i][:, t * 512 : (t + 1) * 512], in_=zp[i, t][:].rearrange("q b c -> q (b c)"), func=ACT.Square, bias=eps[:])
 
+        def sq_shift(i, t):
+            if yt[i] is None:
+                yt[i] = pool.tile([P, 2048], F32, name="yt", tag="yt", bufs=3)
+            nc.vector.tensor_scalar(out=yt[i][:, t * 512 : (t + 1) * 512], in0=zp[i, t][:].rearrange("q b c -> q (b c)"), scalar1=EPS, scalar2=None, op0=ALU.add)
+
+        def sq_mul(i, t0, t1):
+            cols = slice(t0 * 512, t1 * 512)
+            nc.vector.tensor_tensor(out=yt[i][:, cols], in0=yt[i][:, cols], in1=yt[i][:, cols], op=ALU.mult)
+
         def gelu(i, t):
             if gt[i] is None:
                 gt[i] = pool.tile([P, 2048], F32, name="gt", tag="gt", bufs=3)
@@ -295,298 +304,300 @@ def tile_getspatialgatingweights_pa_v_kernel(tc, x_norm, w1_u, b1_u, w2, b2, z, 
 
         with tc.manual_schedule():
             load_z(0, 2, 4)
+            z_trans(0, 3)
             z_trans(0, 2)
             load_z(0, 0, 2)
-            ld_g(0, 2, 4)
-            z_trans(0, 3)
-            heat()
-            load_z(1)
-            ld_g(0, 0, 2)
-            warmup()
             z_trans(0, 0)
-            heat()
+            load_z(1)
+            sq_shift(0, 3)
+            sq_shift(0, 2)
+            sq_shift(0, 0)
             z_trans(0, 1)
-            sq(0, 2)
-            gelu(0, 2)
+            ld_g(0, 2, 4)
             ld_w2()
-            heat()
+            warmup()
+            gelu(0, 3)
             z_trans(1, 2)
             z_trans(1, 0)
-            sq(0, 3)
-            w_inter("w2")
-            heat()
-            ld_g(1, 0, 4)
-            sep_g(0, 0, 2)
-            load_z(2)
-            z_trans(1, 1)
-            sep_g(0, 2, 4)
-            gelu(0, 3)
-            z_trans(1, 3)
+            gelu(0, 2)
             gelu(0, 0)
-            g_trans(0, 1, 0)
+            gelu(0, 1)
+            sq_shift(0, 1)
+            ld_g(0, 0, 2)
+            gelu(1, 2)
+            z_trans(1, 3)
+            sq_mul(0, 0, 2)
+            ld_g(1, 0, 4)
+            sep_g(0, 2, 4)
+            sq_mul(0, 2, 4)
+            sq(1, 2)
+            w_inter("w2")
+            sq(1, 0)
+            gelu(1, 0)
+            g_trans(0, 1, 1)
+            ld_w1()
+            sq(1, 3)
+            sep_g(0, 0, 2)
+            gelu(1, 3)
+            z_trans(1, 1)
+            gelu(1, 1)
+            g_trans(0, 0, 1)
+            g_copy("v", 0, 1, 1)
+            sq(1, 1)
+            load_z(3)
+            sep_g(1, 0, 4)
+            heat()
             heat()
             g_trans(0, 0, 0)
-            sep_g(1, 0, 4)
-            ld_x(0)
-            g_copy("v", 0, 1, 0)
-            g_trans(0, 0, 1)
             g_copy("v", 0, 0, 1)
+            g_trans(0, 1, 0)
             heat()
-            sq(0, 0)
-            gelu(0, 1)
-            sq(0, 1)
-            gelu(1, 2)
-            ld_w1()
-            g_trans(0, 1, 1)
-            heat()
-            g_copy("v", 0, 1, 1)
-            heat()
-            gelu(1, 0)
-            sq(1, 0)
-            sq(1, 2)
-            g_trans(1, 1, 1)
-            g_trans(1, 1, 0)
-            q_g(0, 1)
-            sq(1, 1)
-            sep_x(0)
-            z_trans(2, 0)
+            ld_x(0)
             w2_quant()
             g_copy("v", 0, 0, 0)
-            sq(1, 3)
-            x_trans(0, 0)
-            gelu(1, 1)
-            z_trans(2, 2)
-            gelu(1, 3)
+            heat()
             ln(0)
-            g_copy("v", 1, 1, 1)
+            heat()
+            g_trans(1, 1, 1)
             ln(1)
-            recip(0)
-            w_inter("w1")
             q_g(0, 0)
+            recip(0)
+            g_copy("v", 0, 1, 0)
+            q_g(0, 1)
+            load_z(2)
+            v_m("g", 0, 0, 2)
+            g_trans(1, 0, 0)
             heat()
-            g_copy("v", 1, 1, 0)
-            x_trans(0, 1)
-            v_m("v", 0, 0, 2)
-            v_m("v", 0, 2, 4)
-            heat()
-            load_z(3)
-            recip(1)
+            stage_one(0, 2)
+            g_copy("v", 1, 0, 0)
+            g_copy("v", 1, 1, 1)
             gauss(0)
+            sep_x(0)
+            heat()
+            z_trans(2, 0)
+            z_trans(2, 2)
+            recip(1)
+            heat()
+            heat()
+            heat()
+            w_inter("w1")
+            g_trans(1, 1, 0)
+            x_trans(0, 1)
+            v_m("g", 1, 0, 2)
+            g_copy("v", 1, 1, 0)
+            v_m("v", 0, 2, 4)
+            x_trans(0, 0)
+            sq(2, 0)
+            pe_sum(0, 0)
             gauss(1)
             pe_sum(0, 1)
-            pe_sum(0, 3)
-            g_trans(1, 0, 0)
-            v_m("v", 1, 2, 4)
             pe_sum(0, 2)
-            g_trans(1, 0, 1)
-            stage_one(1, 2)
-            pe_sum(1, 2)
-            x_copy("v", 0)
-            v_dp(0, 1)
-            z_trans(2, 1)
-            sq(2, 0)
-            stage_one(0, 3)
-            q_g(1, 1)
-            w1_quant()
-            z_trans(2, 3)
-            v_dp(0, 2)
-            v_m("v", 1, 0, 2)
-            pe_sum(0, 0)
-            v_dp(0, 3)
-            gelu(2, 0)
-            z_trans(3, 2)
-            g_copy("v", 1, 0, 0)
-            stage_one(0, 1)
-            sq(2, 2)
-            stage_one(0, 0)
-            z_trans(3, 0)
             ld_x(1)
-            stage_one(0, 2)
-            gelu(2, 2)
-            v_dp(1, 2)
-            q_x(0)
-            v_dz(1, 2)
+            g_trans(1, 0, 1)
+            stage_one(0, 0)
+            pe_sum(0, 3)
+            gelu(2, 0)
+            q_g(1, 1)
             v_dp(0, 0)
-            sq(2, 1)
-            g_copy("v", 1, 0, 1)
-            v_dz(0, 3)
-            z_trans(3, 3)
-            v_dz(0, 0)
-            v_dz(0, 1)
-            z_trans(3, 1)
+            gelu(2, 2)
+            stage_one(0, 1)
+            stage_one(0, 3)
+            x_copy("v", 0)
+            v_dp(0, 2)
+            z_trans(2, 3)
             v_dz(0, 2)
-            pe_sum(1, 3)
-            gelu(2, 1)
-            sq(2, 3)
-            gelu(2, 3)
-            sq(3, 2)
-            d_trans(0, 0)
+            g_copy("v", 1, 0, 1)
+            v_dz(0, 0)
+            v_dp(0, 1)
             q_g(1, 0)
-            pe_sum(1, 1)
-            gelu(3, 2)
-            d_trans(0, 1)
-            gelu(3, 0)
-            stage_one(1, 3)
             stage_one(1, 0)
-            pe_sum(1, 0)
-            inter("v", 0)
-            sq(3, 0)
-            v_dp(1, 3)
-            gelu(3, 3)
-            q_o(0)
-            x_trans(1, 1)
-            gelu(3, 1)
-            sq(3, 3)
-            d_copy("v", 0)
-            v_dp(1, 1)
+            z_trans(2, 1)
+            v_dp(0, 3)
+            v_dz(0, 3)
+            sq(2, 2)
+            sq(2, 3)
             stage_one(1, 1)
+            v_m("g", 1, 2, 4)
+            z_trans(3, 2)
+            pe_sum(1, 3)
+            gelu(2, 3)
+            v_dz(0, 1)
+            sq(2, 1)
+            z_trans(3, 0)
+            d_trans(0, 0)
+            z_trans(3, 3)
+            w1_quant()
+            pe_sum(1, 1)
+            inter("v", 0)
+            z_trans(3, 1)
+            q_x(0)
+            q_o(0)
+            v_dp(1, 1)
+            gelu(2, 1)
             sep_x(1)
-            sq(3, 1)
-            ln(2)
-            x_trans(1, 0)
-            q_d(0)
-            x_trans(2, 0)
-            v_dp(1, 0)
-            x_copy("v", 1)
-            v_dz(1, 1)
-            v_dz(1, 3)
-            v_dz(1, 0)
-            x_trans(2, 1)
-            ln(3)
-            mm_out0(0, 0)
-            mm_out0(0, 1)
-            recip(2)
-            gauss(2)
-            out0("s", 0, 0)
-            stage_one(2, 0)
-            q_x(1)
-            v_m("v", 2, 0, 2)
-            v_m("v", 2, 2, 4)
-            stage_one(2, 3)
-            pe_sum(2, 0)
-            pe_sum(2, 3)
-            inter("v", 1)
-            mm_out0(0, 2)
-            d_trans(1, 0)
-            pe_sum(2, 1)
-            pe_sum(2, 2)
-            v_dp(2, 0)
-            d_trans(1, 1)
-            x_copy("s", 2)
-            out0("s", 0, 1)
-            recip(3)
-            v_dp(2, 3)
-            out0("s", 0, 2)
-            v_dz(2, 0)
-            stage_one(2, 1)
-            q_o(1)
-            gauss(3)
-            d_copy("s", 1)
+            v_dp(1, 3)
+            gelu(3, 2)
+            sq(3, 2)
+            pe_sum(1, 2)
+            d_trans(0, 1)
             mm_out0(0, 3)
-            v_dp(2, 1)
-            st0(0, 0)
-            v_dz(2, 3)
+            sq(3, 0)
+            mm_out0(0, 2)
+            pe_sum(1, 0)
+            x_trans(1, 1)
+            stage_one(1, 3)
+            v_dz(1, 1)
+            x_trans(1, 0)
+            gelu(3, 0)
+            gelu(3, 3)
+            d_copy("v", 0)
+            sq(3, 3)
+            mm_out0(0, 0)
+            sq(3, 1)
+            x_trans(2, 0)
+            gelu(3, 1)
+            out0("v", 0, 2)
+            out0("v", 0, 3)
+            ln(2)
+            q_d(0)
+            v_dz(1, 3)
+            x_copy("v", 1)
+            x_trans(2, 1)
+            v_dp(1, 2)
+            ln(3)
+            stage_one(1, 2)
+            recip(2)
+            v_dp(1, 0)
+            out0("v", 0, 0)
+            mm_out0(0, 1)
+            stage_one(2, 1)
+            gauss(2)
+            recip(3)
+            x_copy("v", 2)
+            v_dz(1, 0)
             stage_one(2, 2)
-            v_m("v", 3, 2, 4)
-            v_dz(2, 1)
-            v_dp(2, 2)
-            v_m("v", 3, 0, 2)
-            mm_out0(1, 1)
-            pe_sum(3, 3)
-            v_dz(2, 2)
-            pe_sum(3, 2)
-            q_d(1)
-            d_trans(2, 0)
+            v_m("v", 2, 2, 4)
+            d_trans(1, 0)
+            v_m("g", 2, 0, 2)
+            v_dz(1, 2)
+            out0("v", 0, 1)
+            pe_sum(2, 3)
+            v_dp(2, 3)
+            pe_sum(2, 2)
+            pe_sum(2, 0)
+            d_trans(1, 1)
             q_x(2)
-            pe_sum(3, 1)
-            pe_sum(3, 0)
-            d_trans(2, 1)
-            st0(0, 1)
-            mm_out0(1, 0)
-            out0("s", 0, 3)
-            inter("s", 2)
-            stage_one(3, 2)
-            mm_out0(1, 2)
-            st0(0, 2)
-            out0("s", 1, 1)
-            out0("s", 1, 0)
-            stage_one(3, 3)
-            v_dp(3, 3)
-            v_dp(3, 1)
-            v_dp(3, 2)
-            q_o(2)
-            st0(0, 3)
-            d_copy("s", 2)
-            out0("v", 1, 2)
-            mm_out0(2, 2)
-            stage_one(3, 1)
-            st0(1, 1)
-            v_dp(3, 0)
-            x_trans(3, 0)
-            x_trans(3, 1)
-            v_dz(3, 3)
+            v_dp(2, 2)
+            v_dp(2, 0)
+            st0(0, 0)
+            v_m("g", 3, 0, 2)
+            v_dz(2, 2)
+            stage_one(2, 3)
+            stage_one(2, 0)
+            inter("s", 1)
+            pe_sum(2, 1)
             stage_one(3, 0)
-            mm_out0(2, 0)
-            mm_out1(1, 0)
-            out0("s", 2, 2)
-            st0(1, 0)
-            mm_out0(2, 3)
-            x_copy("s", 3)
-            mm_out1(1, 1)
-            v_dz(3, 2)
-            st0(2, 2)
+            gauss(3)
+            v_dz(2, 3)
+            d_copy("s", 1)
+            q_o(1)
+            v_m("g", 3, 2, 4)
+            mm_out0(1, 1)
+            v_dp(2, 1)
+            v_dz(2, 0)
             mm_out0(1, 3)
-            d_trans(3, 1)
-            out0("s", 2, 0)
-            v_dz(3, 1)
-            v_dz(3, 0)
-            out0("s", 2, 3)
+            v_dz(2, 1)
+            pe_sum(3, 0)
+            out0("v", 1, 1)
+            q_d(1)
+            pe_sum(3, 1)
+            st0(0, 2)
+            d_trans(2, 0)
+            d_trans(2, 1)
+            q_x(1)
+            pe_sum(3, 2)
+            inter("s", 2)
+            v_dp(3, 0)
+            pe_sum(3, 3)
+            v_dp(3, 1)
+            st0(0, 3)
             out0("s", 1, 3)
+            q_o(2)
+            mm_out0(1, 2)
+            st0(0, 1)
+            mm_out0(2, 2)
+            stage_one(3, 2)
+            stage_one(3, 1)
+            stage_one(3, 3)
+            mm_out0(1, 0)
+            st0(1, 1)
+            v_dp(3, 2)
+            st0(1, 3)
+            v_dp(3, 3)
+            d_copy("s", 2)
+            out0("s", 1, 2)
+            x_trans(3, 1)
+            v_dz(3, 0)
+            x_trans(3, 0)
+            v_dz(3, 2)
+            out0("s", 1, 0)
+            v_dz(3, 1)
+            mm_out1(3, 0)
+            v_dz(3, 3)
+            mm_out1(2, 0)
+            mm_out0(2, 3)
             q_d(2)
+            out0("s", 2, 2)
+            x_copy("s", 3)
             inter("v", 3)
+            mm_out0(2, 1)
+            out0("v", 2, 1)
             q_o(3)
             d_trans(3, 0)
-            mm_out1(1, 2)
-            mm_out1(0, 0)
-            st0(2, 0)
-            mm_out0(2, 1)
-            mm_out0(3, 0)
-            mm_out0(3, 3, "tr")
-            out0("v", 2, 1)
-            st0(2, 3)
-            mm_out1(3, 0)
-            mm_out0(3, 1)
-            d_copy("s", 3)
-            q_d(3)
-            out0("s", 3, 0)
-            mm_out0(3, 2, "tr")
-            q_x(3)
-            mm_out1(0, 1)
+            d_trans(3, 1)
+            mm_out0(2, 0)
             mm_out1(3, 1)
-            st0(1, 3)
-            st0(1, 2)
-            out0("v", 3, 2)
+            mm_out0(3, 3, "tr")
             mm_out1(3, 2)
-            mm_out1(3, 3)
+            out0("s", 2, 3)
+            st0(1, 2)
+            d_copy("s", 3)
+            out0("v", 2, 0)
             out0("s", 3, 3)
-            out0("s", 3, 1)
-            out1("s", 3)
-            mm_out1(0, 2)
-            st0(2, 1)
-            st0(3, 0)
-            mm_out1(1, 3)
-            st0(3, 3)
-            mm_out1(0, 3)
-            st0(3, 1)
-            st0(3, 2)
-            mm_out1(2, 0)
-            out1("s", 1)
+            mm_out0(3, 2, "tr")
+            st0(1, 0)
+            mm_out0(3, 1)
+            mm_out0(3, 0)
+            q_x(3)
+            mm_out1(1, 0)
+            st0(2, 2)
             mm_out1(2, 1)
-            out1("s", 0)
+            q_d(3)
+            out0("s", 3, 1)
+            mm_out1(0, 0)
+            out0("s", 3, 0)
+            st0(2, 3)
+            mm_out1(0, 1)
+            mm_out1(3, 3)
             mm_out1(2, 2)
+            st0(2, 1)
             mm_out1(2, 3)
+            out0("v", 3, 2)
+            mm_out1(0, 2)
+            st0(2, 0)
+            mm_out1(0, 3)
+            st0(3, 3)
+            out1("v", 3)
+            st0(3, 1)
+            mm_out1(1, 1)
             out1("v", 2)
+            st0(3, 2)
+            st0(3, 0)
+            mm_out1(1, 2)
+            mm_out1(1, 3)
             st1(3)
-            st1(1)
-            st1(0)
+            out1("s", 0)
             st1(2)
+            out1("v", 1)
+            st1(0)
+            st1(1)

@@ -75,8 +75,8 @@ def tile_getspatialgatingweights_pa_v_kernel(tc, x_norm, w1_u, b1_u, w2, b2, z, 
 
         def w_inter(key):
             wi[key] = pool.tile([P, 2048], BF16, name="wi", tag="wi", bufs=1, align_bytes=64)
-            nc.vector.tensor_copy(out=wi[key][:].rearrange("p (c j) -> p c j", j=4),
-                                  in_=wraw[key][:].rearrange("p (j c) -> p c j", j=4))
+            nc.vector.tensor_copy(out=wi[key][:].rearrange("p (c k j) -> p c j k", j=4, k=4),
+                                  in_=wraw[key][:].rearrange("p (j c k) -> p c j k", j=4, k=4))
 
         def w2_quant():
             for hf in range(2):
@@ -199,8 +199,8 @@ def tile_getspatialgatingweights_pa_v_kernel(tc, x_norm, w1_u, b1_u, w2, b2, z, 
 
         def inter(eng, i):
             dzi[i] = pool.tile([P, 2048], BF16, name="dzi", tag="dzi" + eng, bufs=1, align_bytes=64)
-            dst = dzi[i][:].rearrange("p (c t) -> p c t", t=4)
-            src = dzb[i][:].rearrange("p (t c) -> p c t", t=4)
+            dst = dzi[i][:].rearrange("p (c k t) -> p c t k", t=4, k=4)
+            src = dzb[i][:].rearrange("p (t c k) -> p c t k", t=4, k=4)
             if eng == "v":
                 nc.vector.tensor_copy(out=dst, in_=src)
             else:
@@ -299,305 +299,309 @@ def tile_getspatialgatingweights_pa_v_kernel(tc, x_norm, w1_u, b1_u, w2, b2, z, 
             nc.tensor.matmul(out=hb["t"][:], lhsT=ident[:], rhs=zt[0][:, :256], start=True, stop=True)
 
         def warmup():
-            nc.scalar.activation(out=lnk[:], in_=ones[:], func=ACT.Ln, scale=INV_SQRT_2PI)
             nc.scalar.activation(out=warm[:], in_=eps[:], func=ACT.Gelu)
 
+        def make_lnk():
+            nc.scalar.activation(out=lnk[:], in_=ones[:], func=ACT.Ln, scale=INV_SQRT_2PI)
+
         with tc.manual_schedule():
-            load_z(0, 2, 4)
+            make_lnk()
+            load_z(0, 2, 3)
+            warmup()
+            load_z(0, 3, 4)
             z_trans(0, 3)
             z_trans(0, 2)
             load_z(0, 0, 2)
+            gelu(0, 3)
+            gelu(0, 2)
+            heat()
             z_trans(0, 0)
+            gelu(0, 0)
             load_z(1)
+            z_trans(0, 1)
             sq_shift(0, 3)
             sq_shift(0, 2)
             sq_shift(0, 0)
-            z_trans(0, 1)
-            ld_g(0, 2, 4)
-            ld_w2()
-            warmup()
-            gelu(0, 3)
             z_trans(1, 2)
-            z_trans(1, 0)
-            gelu(0, 2)
-            gelu(0, 0)
+            z_trans(1, 1)
             gelu(0, 1)
             sq_shift(0, 1)
-            ld_g(0, 0, 2)
-            gelu(1, 2)
-            z_trans(1, 3)
-            sq_mul(0, 0, 2)
-            ld_g(1, 0, 4)
-            sep_g(0, 2, 4)
-            sq_mul(0, 2, 4)
             sq(1, 2)
-            w_inter("w2")
+            gelu(1, 2)
+            sq_mul(0, 2, 4)
+            sq(1, 1)
+            z_trans(1, 3)
+            ld_g(0, 0, 2)
+            z_trans(1, 0)
+            sq_mul(0, 0, 2)
+            ld_g(0, 2, 4)
+            ld_w2()
+            sep_g(0, 2, 4)
+            sep_g(0, 0, 2)
+            gelu(1, 1)
+            sq(1, 3)
+            gelu(1, 3)
             sq(1, 0)
             gelu(1, 0)
-            g_trans(0, 1, 1)
-            ld_w1()
-            sq(1, 3)
-            sep_g(0, 0, 2)
-            gelu(1, 3)
-            z_trans(1, 1)
-            gelu(1, 1)
-            g_trans(0, 0, 1)
-            g_copy("v", 0, 1, 1)
-            sq(1, 1)
-            load_z(3)
-            sep_g(1, 0, 4)
-            heat()
-            heat()
-            g_trans(0, 0, 0)
-            g_copy("v", 0, 0, 1)
             g_trans(0, 1, 0)
-            heat()
+            w_inter("w2")
+            g_trans(0, 1, 1)
+            g_trans(0, 0, 0)
+            g_trans(0, 0, 1)
+            ld_w1()
             ld_x(0)
+            ld_g(1, 0, 4)
+            g_copy("v", 0, 1, 0)
+            g_copy("v", 0, 1, 1)
             w2_quant()
             g_copy("v", 0, 0, 0)
-            heat()
-            ln(0)
-            heat()
-            g_trans(1, 1, 1)
-            ln(1)
-            q_g(0, 0)
-            recip(0)
-            g_copy("v", 0, 1, 0)
             q_g(0, 1)
+            heat()
+            g_copy("v", 0, 0, 1)
+            heat()
+            sep_g(1, 0, 4)
             load_z(2)
-            v_m("g", 0, 0, 2)
-            g_trans(1, 0, 0)
+            g_trans(1, 1, 1)
             heat()
-            stage_one(0, 2)
-            g_copy("v", 1, 0, 0)
-            g_copy("v", 1, 1, 1)
-            gauss(0)
-            sep_x(0)
-            heat()
-            z_trans(2, 0)
-            z_trans(2, 2)
-            recip(1)
-            heat()
-            heat()
+            g_trans(1, 1, 0)
             heat()
             w_inter("w1")
-            g_trans(1, 1, 0)
-            x_trans(0, 1)
-            v_m("g", 1, 0, 2)
+            q_g(0, 0)
+            heat()
+            z_trans(2, 0)
+            heat()
+            heat()
+            g_copy("v", 1, 1, 1)
             g_copy("v", 1, 1, 0)
-            v_m("v", 0, 2, 4)
+            w1_quant()
+            sep_x(0)
+            stage_one(0, 2)
+            heat()
+            ln(0)
+            ln(1)
+            x_trans(0, 1)
+            stage_one(0, 0)
             x_trans(0, 0)
-            sq(2, 0)
+            recip(0)
+            v_m("v", 0, 2, 4)
+            v_m("v", 0, 0, 2)
+            gauss(0)
+            q_g(1, 1)
+            x_copy("v", 0)
             pe_sum(0, 0)
+            heat()
+            recip(1)
             gauss(1)
-            pe_sum(0, 1)
+            pe_sum(0, 3)
+            z_trans(2, 2)
             pe_sum(0, 2)
             ld_x(1)
-            g_trans(1, 0, 1)
-            stage_one(0, 0)
-            pe_sum(0, 3)
+            load_z(3)
+            sq(2, 0)
             gelu(2, 0)
-            q_g(1, 1)
             v_dp(0, 0)
+            v_m("v", 1, 2, 4)
             gelu(2, 2)
+            sq(2, 2)
+            g_trans(1, 0, 1)
+            g_trans(1, 0, 0)
+            pe_sum(0, 1)
+            z_trans(2, 3)
+            sq(2, 3)
+            v_dp(0, 3)
+            gelu(2, 3)
+            v_dp(0, 2)
             stage_one(0, 1)
             stage_one(0, 3)
-            x_copy("v", 0)
-            v_dp(0, 2)
-            z_trans(2, 3)
-            v_dz(0, 2)
+            z_trans(3, 2)
             g_copy("v", 1, 0, 1)
             v_dz(0, 0)
-            v_dp(0, 1)
-            q_g(1, 0)
-            stage_one(1, 0)
-            z_trans(2, 1)
-            v_dp(0, 3)
-            v_dz(0, 3)
-            sq(2, 2)
-            sq(2, 3)
-            stage_one(1, 1)
-            v_m("g", 1, 2, 4)
-            z_trans(3, 2)
-            pe_sum(1, 3)
-            gelu(2, 3)
-            v_dz(0, 1)
-            sq(2, 1)
-            z_trans(3, 0)
-            d_trans(0, 0)
-            z_trans(3, 3)
-            w1_quant()
-            pe_sum(1, 1)
-            inter("v", 0)
-            z_trans(3, 1)
-            q_x(0)
-            q_o(0)
-            v_dp(1, 1)
-            gelu(2, 1)
-            sep_x(1)
-            v_dp(1, 3)
             gelu(3, 2)
+            v_dp(0, 1)
+            v_dz(0, 2)
+            v_m("v", 1, 0, 2)
             sq(3, 2)
+            v_dz(0, 3)
+            v_dz(0, 1)
+            z_trans(3, 0)
+            g_copy("v", 1, 0, 0)
             pe_sum(1, 2)
-            d_trans(0, 1)
-            mm_out0(0, 3)
-            sq(3, 0)
-            mm_out0(0, 2)
+            z_trans(2, 1)
             pe_sum(1, 0)
-            x_trans(1, 1)
-            stage_one(1, 3)
-            v_dz(1, 1)
-            x_trans(1, 0)
-            gelu(3, 0)
-            gelu(3, 3)
-            d_copy("v", 0)
-            sq(3, 3)
-            mm_out0(0, 0)
-            sq(3, 1)
-            x_trans(2, 0)
-            gelu(3, 1)
-            out0("v", 0, 2)
-            out0("v", 0, 3)
-            ln(2)
-            q_d(0)
-            v_dz(1, 3)
-            x_copy("v", 1)
-            x_trans(2, 1)
-            v_dp(1, 2)
-            ln(3)
-            stage_one(1, 2)
-            recip(2)
+            z_trans(3, 3)
+            inter("v", 0)
             v_dp(1, 0)
-            out0("v", 0, 0)
-            mm_out0(0, 1)
-            stage_one(2, 1)
-            gauss(2)
-            recip(3)
-            x_copy("v", 2)
-            v_dz(1, 0)
-            stage_one(2, 2)
-            v_m("v", 2, 2, 4)
-            d_trans(1, 0)
-            v_m("g", 2, 0, 2)
-            v_dz(1, 2)
-            out0("v", 0, 1)
-            pe_sum(2, 3)
-            v_dp(2, 3)
-            pe_sum(2, 2)
-            pe_sum(2, 0)
-            d_trans(1, 1)
-            q_x(2)
-            v_dp(2, 2)
-            v_dp(2, 0)
-            st0(0, 0)
-            v_m("g", 3, 0, 2)
-            v_dz(2, 2)
+            q_o(0)
+            sep_x(1)
+            pe_sum(1, 3)
+            sq(3, 0)
+            gelu(3, 0)
+            z_trans(3, 1)
+            sq(2, 1)
+            gelu(2, 1)
+            d_trans(0, 1)
+            q_g(1, 0)
+            pe_sum(1, 1)
+            mm_out0(0, 0)
+            d_trans(0, 0)
+            stage_one(1, 3)
+            mm_out0(0, 2)
+            stage_one(1, 0)
+            x_trans(1, 1)
+            x_trans(1, 0)
+            sq(3, 3)
+            gelu(3, 3)
+            gelu(3, 1)
+            sq(3, 1)
+            v_dp(1, 1)
+            v_dp(1, 3)
+            stage_one(1, 2)
+            ln(2)
             stage_one(2, 3)
+            mm_out0(0, 1)
+            ln(3)
+            mm_out0(0, 3)
+            stage_one(1, 1)
+            x_trans(2, 1)
             stage_one(2, 0)
-            inter("s", 1)
-            pe_sum(2, 1)
-            stage_one(3, 0)
-            gauss(3)
-            v_dz(2, 3)
-            d_copy("s", 1)
-            q_o(1)
-            v_m("g", 3, 2, 4)
-            mm_out0(1, 1)
-            v_dp(2, 1)
-            v_dz(2, 0)
-            mm_out0(1, 3)
-            v_dz(2, 1)
-            pe_sum(3, 0)
-            out0("v", 1, 1)
-            q_d(1)
-            pe_sum(3, 1)
-            st0(0, 2)
-            d_trans(2, 0)
-            d_trans(2, 1)
+            d_copy("v", 0)
+            v_dp(1, 2)
+            recip(2)
+            q_x(0)
+            v_dz(1, 2)
+            out0("v", 0, 2)
+            x_copy("v", 1)
+            out0("v", 0, 1)
+            x_trans(2, 0)
             q_x(1)
-            pe_sum(3, 2)
-            inter("s", 2)
-            v_dp(3, 0)
-            pe_sum(3, 3)
-            v_dp(3, 1)
+            gauss(2)
+            v_dz(1, 3)
+            q_d(0)
+            v_dz(1, 0)
+            recip(3)
+            out0("s", 0, 3)
+            x_copy("s", 2)
+            v_m("v", 2, 2, 4)
+            v_dz(1, 1)
+            pe_sum(2, 3)
+            pe_sum(2, 2)
+            v_m("v", 2, 0, 2)
+            pe_sum(2, 0)
+            pe_sum(2, 1)
+            v_dp(2, 3)
+            v_dp(2, 2)
+            gauss(3)
+            d_trans(1, 0)
+            inter("s", 1)
+            stage_one(2, 2)
+            stage_one(2, 1)
+            v_m("v", 3, 0, 2)
+            v_dz(2, 3)
             st0(0, 3)
-            out0("s", 1, 3)
-            q_o(2)
-            mm_out0(1, 2)
-            st0(0, 1)
-            mm_out0(2, 2)
-            stage_one(3, 2)
+            v_dp(2, 0)
+            v_dp(2, 1)
+            pe_sum(3, 1)
+            d_trans(1, 1)
+            v_dz(2, 0)
+            v_m("v", 3, 2, 4)
+            pe_sum(3, 3)
+            pe_sum(3, 2)
+            v_dz(2, 2)
+            v_dz(2, 1)
+            q_o(1)
+            mm_out0(1, 1)
+            mm_out1(0, 0)
+            mm_out0(1, 3)
             stage_one(3, 1)
-            stage_one(3, 3)
-            mm_out0(1, 0)
-            st0(1, 1)
+            stage_one(3, 2)
+            out0("s", 0, 0)
+            d_copy("s", 1)
+            mm_out0(1, 2)
+            v_dp(3, 1)
+            d_trans(2, 1)
+            pe_sum(3, 0)
             v_dp(3, 2)
-            st0(1, 3)
             v_dp(3, 3)
-            d_copy("s", 2)
-            out0("s", 1, 2)
-            x_trans(3, 1)
-            v_dz(3, 0)
-            x_trans(3, 0)
-            v_dz(3, 2)
-            out0("s", 1, 0)
+            d_trans(2, 0)
+            out0("s", 1, 1)
             v_dz(3, 1)
-            mm_out1(3, 0)
+            q_x(2)
+            stage_one(3, 0)
+            out0("s", 1, 3)
+            inter("s", 2)
+            v_dz(3, 2)
+            q_d(1)
+            v_dp(3, 0)
+            mm_out0(1, 0)
+            stage_one(3, 3)
+            q_o(2)
+            v_dz(3, 0)
             v_dz(3, 3)
-            mm_out1(2, 0)
-            mm_out0(2, 3)
+            out0("s", 1, 2)
+            mm_out0(2, 0)
+            d_copy("s", 2)
+            x_trans(3, 0)
+            x_trans(3, 1)
+            mm_out1(1, 0)
+            out0("s", 1, 0)
+            st0(0, 0)
             q_d(2)
-            out0("s", 2, 2)
-            x_copy("s", 3)
+            st0(1, 1)
             inter("v", 3)
+            st0(1, 3)
             mm_out0(2, 1)
+            mm_out0(2, 2)
+            out0("s", 2, 0)
+            st0(0, 2)
+            st0(0, 1)
+            st0(1, 2)
+            x_copy("s", 3)
+            st0(2, 0)
+            st0(1, 0)
+            out0("s", 2, 2)
             out0("v", 2, 1)
-            q_o(3)
             d_trans(3, 0)
             d_trans(3, 1)
-            mm_out0(2, 0)
-            mm_out1(3, 1)
-            mm_out0(3, 3, "tr")
-            mm_out1(3, 2)
-            out0("s", 2, 3)
-            st0(1, 2)
+            mm_out0(2, 3)
+            q_o(3)
+            mm_out1(2, 0)
+            mm_out1(3, 0)
             d_copy("s", 3)
-            out0("v", 2, 0)
-            out0("s", 3, 3)
             mm_out0(3, 2, "tr")
-            st0(1, 0)
-            mm_out0(3, 1)
+            out0("v", 2, 3)
+            mm_out1(3, 1)
             mm_out0(3, 0)
+            mm_out0(3, 3, "tr")
+            out0("s", 3, 2)
             q_x(3)
-            mm_out1(1, 0)
-            st0(2, 2)
-            mm_out1(2, 1)
             q_d(3)
-            out0("s", 3, 1)
-            mm_out1(0, 0)
+            st0(2, 2)
             out0("s", 3, 0)
-            st0(2, 3)
-            mm_out1(0, 1)
-            mm_out1(3, 3)
-            mm_out1(2, 2)
             st0(2, 1)
-            mm_out1(2, 3)
-            out0("v", 3, 2)
+            mm_out1(0, 1)
+            mm_out0(3, 1)
+            mm_out1(2, 1)
+            out0("s", 3, 1)
+            mm_out1(3, 2)
+            st0(2, 3)
+            out0("v", 3, 3)
+            mm_out1(3, 3)
             mm_out1(0, 2)
-            st0(2, 0)
-            mm_out1(0, 3)
-            st0(3, 3)
             out1("v", 3)
-            st0(3, 1)
-            mm_out1(1, 1)
-            out1("v", 2)
+            mm_out1(0, 3)
             st0(3, 2)
             st0(3, 0)
+            mm_out1(2, 2)
+            mm_out1(2, 3)
+            mm_out1(1, 1)
+            st0(3, 3)
             mm_out1(1, 2)
+            st0(3, 1)
             mm_out1(1, 3)
+            out1("v", 0)
+            out1("s", 2)
             st1(3)
-            out1("s", 0)
-            st1(2)
-            out1("v", 1)
+            out1("s", 1)
             st1(0)
+            st1(2)
             st1(1)

from contextlib import ExitStack

import concourse.mybir as mybir
from concourse.masks import make_identity

F32 = mybir.dt.float32
BF16 = mybir.dt.bfloat16
U32 = mybir.dt.uint32
U8 = mybir.dt.uint8
E4 = mybir.dt.float8_e4m3fn_x4
E5 = mybir.dt.float8_e5m2_x4
ACT = mybir.ActivationFunctionType
ALU = mybir.AluOpType

P = 128
FLOPS = 3 * 2 * 2048 * 512 * 512
BYTES = (2 + 4 + 2 + 1 + 4 + 1) * 1024 * 1024
EPS = 2.0 ** -31
INV_SQRT_2PI = 0.3989422804014326779399460599343819


def tile_getspatialgatingweights_pa_v_kernel(tc, x_norm, w1_u, b1_u, w2, b2, z, grad_out, out_0, out_1):
    nc = tc.nc
    z_v = z.rearrange("n (p t) d h w -> n p t (d h w)", t=4)
    g_v = grad_out.rearrange("n (p t) d h w -> n p t (d h w)", t=4)
    x_v = x_norm.rearrange("n (j p) d h w -> n p j (d h w)", p=P)
    w1_v = w1_u.rearrange("(p j) c -> p j c", j=4)
    w2_v = w2.rearrange("(p j) c -> p j c", j=4)
    o0_v = out_0.rearrange("n c d h w -> n c (d h w)")
    o1_v = out_1.rearrange("(p t) c -> p t c", t=4)

    with ExitStack() as ctx:
        keep = ctx.enter_context(tc.tile_pool(name="keep", bufs=1))
        pool = ctx.enter_context(tc.tile_pool(name="pool", bufs=1))
        ps = ctx.enter_context(tc.psum_pool(name="ps", bufs=1))

        ident = keep.tile([P, P], F32, name="ident")
        make_identity(nc, ident[:])
        ones = keep.tile([P, 1], F32, name="ones")
        nc.gpsimd.memset(ones[:], 1.0)
        lnk = keep.tile([P, 1], F32, name="lnk")
        eps = keep.tile([P, 1], F32, name="eps")
        nc.gpsimd.memset(eps[:], EPS)
        warm = keep.tile([P, 1], F32, name="warm")
        w2q = keep.tile([P, 1280], U32, name="w2q", align_bytes=64)
        w2s = keep.tile([P, 1280], U8, name="w2s", align_bytes=64)
        nc.gpsimd.memset(w2q[:], 0)
        nc.gpsimd.memset(w2s[:].bitcast(U32), 0)
        w1q = keep.tile([P, 512], U32, name="w1q", align_bytes=64)
        w1s = keep.tile([P, 512], U8, name="w1s", align_bytes=64)

        zt, gt, yt, lt = [None] * 4, [None] * 4, [None] * 4, [None] * 4
        raw, deint = {}, {}
        gq, xq, dq, oq = {}, {}, {}, {}
        ks, dzb, dzi = {}, {}, {}
        tr, du, po, sp, zp, hb = {}, {}, {}, {}, {}, {}
        wraw, wi, ost = {}, {}, {}

        def load_z(i, t0=0, t1=4):
            n, hf = i // 2, i % 2
            if zt[i] is None:
                zt[i] = pool.tile([P, 2048], F32, name="zt", tag="zt", bufs=4)
            nc.sync.dma_start(
                out=zt[i][:, t0 * 512 : t1 * 512].rearrange("p (t x) -> p t x", t=t1 - t0),
                in_=z_v[n, :, t0:t1, hf * 512 : (hf + 1) * 512])

        def load_raw(key, view, n, t0=0, t1=4):
            if key not in raw:
                raw[key] = pool.tile([P, 4096], BF16, name="raw", tag="raw", bufs=2)
            nc.sync.dma_start(out=raw[key][:, t0 * 1024 : t1 * 1024].rearrange("p (t x) -> p t x", t=t1 - t0), in_=view[n, :, t0:t1, :])

        def load_w(key, view):
            wraw[key] = pool.tile([P, 2048], BF16, name="wraw", tag="wraw", bufs=2)
            nc.sync.dma_start(out=wraw[key][:].rearrange("p (j c) -> p j c", j=4), in_=view)

        def w_inter(key):
            wi[key] = pool.tile([P, 2048], BF16, name="wi", tag="wi", bufs=1, align_bytes=64)
            nc.vector.tensor_copy(out=wi[key][:].rearrange("p (c k j) -> p c j k", j=4, k=4),
                                  in_=wraw[key][:].rearrange("p (j c k) -> p c j k", j=4, k=4))

        def w2_quant():
            for hf in range(2):
                lo = 256 + 512 * hf
                nc.vector.quantize_mx(out=w2q[:, lo : lo + 256].bitcast(E4), scales=w2s[:, lo : lo + 256],
                                      in_=wi["w2"][:, hf * 1024 : (hf + 1) * 1024])

        def w1_quant():
            nc.vector.quantize_mx(out=w1q[:].bitcast(E4), scales=w1s[:], in_=wi["w1"][:])

        def separate(key, halves, t0=0, t1=4):
            if key not in deint:
                deint[key] = pool.tile([P, 4096], BF16, name="deint", tag="deint", bufs=2)
            t, a = (t1 - t0) * halves, 64 // halves
            words = slice(t0 * 512, t1 * 512)
            nc.vector.tensor_copy(
                out=deint[key][:].bitcast(F32)[:, words].rearrange("q (t p a w) -> q t p a w", t=t, p=2, a=a, w=4),
                in_=raw[key][:].bitcast(F32)[:, words].rearrange("q (t a p w) -> q t p a w", t=t, p=2, a=a, w=4))

        def transpose_bank(key, words, bases):
            tr[key] = ps.tile([P, 2, 2, P], F32, name="tr", tag="tr", bufs=2)
            for s, base in enumerate(bases):
                for u in range(2):
                    nc.tensor.transpose(tr[key][:, s, u, :], words[:, base + u : base + 256 : 2], ident[:])

        def copy_bank(eng, key, dst, b):
            words = dst[:].bitcast(F32)[:, b * 512 : (b + 1) * 512].rearrange("p (s c u) -> p s c u", s=2, u=2)
            src = tr.pop(key)[:].rearrange("p s u c -> p s c u")
            if eng == "v":
                nc.vector.tensor_copy(out=words, in_=src)
            else:
                nc.scalar.copy(out=words, in_=src)

        def new_ks(key, eng):
            ks[key] = pool.tile([P, 2048], BF16, name="k" + eng, tag="k" + eng, bufs=2, align_bytes=64)

        def g_trans(n, p, b):
            transpose_bank(("g", n, p, b), deint["g", n][:].bitcast(F32), [((2 * b + s) * 2 + p) * 256 for s in range(2)])

        def x_trans(i, b):
            n, hf = i // 2, i % 2
            transpose_bank(("x", n, hf, b), deint["x", n][:].bitcast(F32), [((2 * b + s) * 2 + hf) * 256 for s in range(2)])

        def d_trans(i, b):
            transpose_bank(("d", i, b), dzb[i][:].bitcast(F32), [(2 * b + s) * 256 for s in range(2)])

        def quant(store, key, name, src, fmt, bufs):
            c = pool.tile([P, 512], U32, name=name + "c", tag=name + "c", bufs=bufs, align_bytes=64)
            s = pool.tile([P, 512], U8, name=name + "s", tag=name + "s", bufs=bufs, align_bytes=64)
            nc.vector.quantize_mx(out=c[:].bitcast(fmt), scales=s[:], in_=src[:])
            store[key] = (c, s)

        def stage_one(i, t):
            n, hf = i // 2, i % 2
            du[i, t] = ps.tile([P, 512], F32, name="mm", tag="mm", bufs=4)
            for p in range(2):
                lo = 512 * hf + (256 if p == 0 else 0)
                c, s = gq[n, p]
                nc.tensor.matmul_mx(out=du[i, t][:], lhsT=c[:, t * P : (t + 1) * P].bitcast(E5), lhsT_scale=s[:, t * P : (t + 1) * P],
                                    rhs=w2q[:, lo : lo + 512].bitcast(E4), rhs_scale=w2s[:, lo : lo + 512],
                                    start=(p == 0), stop=(p == 1))

        def ln(i):
            lt[i] = pool.tile([P, 2048], F32, name="lt", tag="lt", bufs=3)
            nc.scalar.activation(out=lt[i][:], in_=yt[i][:], func=ACT.Ln)

        def recip(i):
            nc.scalar.activation(out=lt[i][:], in_=lt[i][:], func=ACT.Exp, scale=-1.0)

        def v_m(eng, i, t0, t1):
            cols = slice(t0 * 512, t1 * 512)
            (nc.vector if eng == "v" else nc.gpsimd).tensor_tensor(out=gt[i][:, cols], in0=gt[i][:, cols], in1=lt[i][:, cols], op=ALU.mult)

        def z_trans(i, t):
            zp[i, t] = ps.tile([P, 4, P], F32, name="po", tag="po", bufs=2)
            for b in range(4):
                nc.tensor.transpose(zp[i, t][:, b, :], zt[i][:, t * 512 + b * P : t * 512 + b * P + P], ident[:])

        def sq(i, t):
            if yt[i] is None:
                yt[i] = pool.tile([P, 2048], F32, name="yt", tag="yt", bufs=3)
            nc.scalar.activation(out=yt[i][:, t * 512 : (t + 1) * 512], in_=zp[i, t][:].rearrange("q b c -> q (b c)"), func=ACT.Square, bias=eps[:])

        def sq_shift(i, t):
            if yt[i] is None:
                yt[i] = pool.tile([P, 2048], F32, name="yt", tag="yt", bufs=3)
            nc.vector.tensor_scalar(out=yt[i][:, t * 512 : (t + 1) * 512], in0=zp[i, t][:].rearrange("q b c -> q (b c)"), scalar1=EPS, scalar2=None, op0=ALU.add)

        def sq_mul(i, t0, t1):
            cols = slice(t0 * 512, t1 * 512)
            nc.vector.tensor_tensor(out=yt[i][:, cols], in0=yt[i][:, cols], in1=yt[i][:, cols], op=ALU.mult)

        def gelu(i, t):
            if gt[i] is None:
                gt[i] = pool.tile([P, 2048], F32, name="gt", tag="gt", bufs=3)
            nc.scalar.activation(out=gt[i][:, t * 512 : (t + 1) * 512], in_=zp[i, t][:].rearrange("q b c -> q (b c)"), func=ACT.Gelu, bias=eps[:])

        def gauss(i):
            nc.scalar.activation(out=yt[i][:], in_=yt[i][:], func=ACT.Exp, scale=-0.5, bias=lnk[:])

        def pe_sum(i, t):
            sp[i, t] = ps.tile([P, 512], F32, name="mm", tag="mm", bufs=4)
            for k, src in enumerate((gt[i], yt[i])):
                for b in range(4):
                    nc.tensor.matmul(out=sp[i, t][:, b * P : b * P + P], lhsT=src[:, t * 512 + b * P : t * 512 + b * P + P], rhs=ident[:],
                                     is_transpose=(k == 1 or b >= 2), start=(k == 0 and b == 0), stop=(k == 1 and b == 3))

        def v_dp(i, t):
            cols = slice(t * 512, (t + 1) * 512)
            nc.vector.scalar_tensor_tensor(out=zt[i][:, cols], in0=zt[i][:, cols], scalar=EPS, in1=sp.pop((i, t))[:], op0=ALU.add, op1=ALU.mult)

        def v_dz(i, t):
            if i not in dzb:
                dzb[i] = pool.tile([P, 2048], BF16, name="dzb", tag="dzb", bufs=2)
            nc.vector.tensor_tensor(
                out=dzb[i][:, t * 512 : (t + 1) * 512].rearrange("q (p a w) -> q p a w", p=2, w=8),
                in0=du.pop((i, t))[:].rearrange("q (p a w) -> q p a w", p=2, w=8),
                in1=zt[i][:, t * 512 : (t + 1) * 512].rearrange("q (a p w) -> q p a w", p=2, w=8),
                op=ALU.mult)

        def inter(eng, i):
            dzi[i] = pool.tile([P, 2048], BF16, name="dzi", tag="dzi" + eng, bufs=1, align_bytes=64)
            dst = dzi[i][:].rearrange("p (c k t) -> p c t k", t=4, k=4)
            src = dzb[i][:].rearrange("p (t c k) -> p c t k", t=4, k=4)
            if eng == "v":
                nc.vector.tensor_copy(out=dst, in_=src)
            else:
                nc.scalar.copy(out=dst, in_=src)

        def mm_out0(i, cc, tag="po"):
            po[i, cc] = ps.tile([P, 512], F32, name="po", tag=tag, bufs=2)
            c, s = oq[i]
            nc.tensor.matmul_mx(out=po[i, cc][:], lhsT=w1q[:, cc * P : (cc + 1) * P].bitcast(E4), lhsT_scale=w1s[:, cc * P : (cc + 1) * P],
                                rhs=c[:].bitcast(E5), rhs_scale=s[:], start=True, stop=True)

        def out0(eng, i, cc):
            o = pool.tile([P, 512], F32, name="ost", tag="ost" + eng, bufs=3)
            dst = o[:].rearrange("q (a p w) -> q p a w", p=2, w=8)
            src = po.pop((i, cc))[:].rearrange("q (p a w) -> q p a w", p=2, w=8)
            if eng == "v":
                nc.vector.tensor_copy(out=dst, in_=src)
            else:
                nc.scalar.copy(out=dst, in_=src)
            ost[i, cc] = o

        def st0(i, cc):
            n, hf = i // 2, i % 2
            nc.sync.dma_start(out=o0_v[n, cc * P : (cc + 1) * P, hf * 512 : (hf + 1) * 512], in_=ost.pop((i, cc))[:])

        o1, o1s = {}, {}

        def mm_out1(t, i):
            if t not in o1:
                o1[t] = ps.tile([P, 512], F32, name="mm", tag="mm", bufs=4)
            dc, ds = dq[i]
            xc, xs = xq[i]
            nc.tensor.matmul_mx(out=o1[t][:], lhsT=dc[:, t * P : (t + 1) * P].bitcast(E5), lhsT_scale=ds[:, t * P : (t + 1) * P],
                                rhs=xc[:].bitcast(E4), rhs_scale=xs[:], start=(i == 0), stop=(i == 3))

        def out1(eng, t):
            if t // 2 not in o1s:
                o1s[t // 2] = pool.tile([P, 1024], F32, name="o1s", tag="raw", bufs=2)
            o = o1s[t // 2][:, (t % 2) * 512 : (t % 2) * 512 + 512]
            if eng == "v":
                nc.vector.tensor_copy(out=o, in_=o1[t][:])
            else:
                nc.scalar.copy(out=o, in_=o1[t][:])

        def st1(t):
            nc.sync.dma_start(out=o1_v[:, t, :], in_=o1s[t // 2][:, (t % 2) * 512 : (t % 2) * 512 + 512])

        def g_copy(eng, n, p, b):
            if ("g", n, p) not in ks:
                new_ks(("g", n, p), eng)
            copy_bank(eng, ("g", n, p, b), ks["g", n, p], b)

        def x_copy(eng, i):
            new_ks(("x", i), eng)
            for b in range(2):
                copy_bank(eng, ("x", i // 2, i % 2, b), ks["x", i], b)

        def d_copy(eng, i):
            new_ks(("d", i), eng)
            for b in range(2):
                copy_bank(eng, ("d", i, b), ks["d", i], b)

        def q_g(n, p):
            quant(gq, (n, p), "gq", ks["g", n, p], E5, 4)

        def q_x(i):
            quant(xq, i, "xq", ks["x", i], E4, 4)

        def q_o(i):
            quant(oq, i, "oq", dzi[i], E5, 2)

        def q_d(i):
            quant(dq, i, "dq", ks["d", i], E5, 4)

        def sep_g(n, t0, t1):
            separate(("g", n), 1, t0, t1)

        def sep_x(n):
            separate(("x", n), 2)

        def ld_g(n, t0, t1):
            load_raw(("g", n), g_v, n, t0, t1)

        def ld_x(n):
            load_raw(("x", n), x_v, n)

        def ld_w2():
            load_w("w2", w2_v)

        def ld_w1():
            load_w("w1", w1_v)

        def heat():
            if "t" not in hb:
                hb["t"] = ps.tile([P, 256], F32, name="mm", tag="mm", bufs=4)
            nc.tensor.matmul(out=hb["t"][:], lhsT=ident[:], rhs=zt[0][:, :256], start=True, stop=True)

        def warmup():
            nc.scalar.activation(out=warm[:], in_=eps[:], func=ACT.Gelu)

        def make_lnk():
            nc.scalar.activation(out=lnk[:], in_=ones[:], func=ACT.Ln, scale=INV_SQRT_2PI)

        with tc.manual_schedule():
            make_lnk()
            load_z(0, 2, 3)
            warmup()
            load_z(0, 3, 4)
            z_trans(0, 3)
            z_trans(0, 2)
            load_z(0, 0, 2)
            gelu(0, 3)
            gelu(0, 2)
            heat()
            z_trans(0, 0)
            gelu(0, 0)
            load_z(1)
            z_trans(0, 1)
            sq_shift(0, 3)
            sq_shift(0, 2)
            sq_shift(0, 0)
            z_trans(1, 2)
            z_trans(1, 1)
            gelu(0, 1)
            sq_shift(0, 1)
            sq(1, 2)
            gelu(1, 2)
            sq_mul(0, 2, 4)
            sq(1, 1)
            z_trans(1, 3)
            ld_g(0, 0, 2)
            z_trans(1, 0)
            sq_mul(0, 0, 2)
            ld_g(0, 2, 4)
            ld_w2()
            sep_g(0, 2, 4)
            sep_g(0, 0, 2)
            gelu(1, 1)
            sq(1, 3)
            gelu(1, 3)
            sq(1, 0)
            gelu(1, 0)
            g_trans(0, 1, 0)
            w_inter("w2")
            g_trans(0, 1, 1)
            g_trans(0, 0, 0)
            g_trans(0, 0, 1)
            ld_w1()
            ld_x(0)
            ld_g(1, 0, 4)
            g_copy("v", 0, 1, 0)
            g_copy("v", 0, 1, 1)
            w2_quant()
            g_copy("v", 0, 0, 0)
            q_g(0, 1)
            heat()
            g_copy("v", 0, 0, 1)
            heat()
            sep_g(1, 0, 4)
            load_z(2)
            g_trans(1, 1, 1)
            heat()
            g_trans(1, 1, 0)
            heat()
            w_inter("w1")
            q_g(0, 0)
            heat()
            z_trans(2, 0)
            heat()
            heat()
            g_copy("v", 1, 1, 1)
            g_copy("v", 1, 1, 0)
            w1_quant()
            sep_x(0)
            stage_one(0, 2)
            heat()
            ln(0)
            ln(1)
            x_trans(0, 1)
            stage_one(0, 0)
            x_trans(0, 0)
            recip(0)
            v_m("v", 0, 2, 4)
            v_m("v", 0, 0, 2)
            gauss(0)
            q_g(1, 1)
            x_copy("v", 0)
            pe_sum(0, 0)
            heat()
            recip(1)
            gauss(1)
            pe_sum(0, 3)
            z_trans(2, 2)
            pe_sum(0, 2)
            ld_x(1)
            load_z(3)
            sq(2, 0)
            gelu(2, 0)
            v_dp(0, 0)
            v_m("v", 1, 2, 4)
            gelu(2, 2)
            sq(2, 2)
            g_trans(1, 0, 1)
            g_trans(1, 0, 0)
            pe_sum(0, 1)
            z_trans(2, 3)
            sq(2, 3)
            v_dp(0, 3)
            gelu(2, 3)
            v_dp(0, 2)
            stage_one(0, 1)
            stage_one(0, 3)
            z_trans(3, 2)
            g_copy("v", 1, 0, 1)
            v_dz(0, 0)
            gelu(3, 2)
            v_dp(0, 1)
            v_dz(0, 2)
            v_m("v", 1, 0, 2)
            sq(3, 2)
            v_dz(0, 3)
            v_dz(0, 1)
            z_trans(3, 0)
            g_copy("v", 1, 0, 0)
            pe_sum(1, 2)
            z_trans(2, 1)
            pe_sum(1, 0)
            z_trans(3, 3)
            inter("v", 0)
            v_dp(1, 0)
            q_o(0)
            sep_x(1)
            pe_sum(1, 3)
            sq(3, 0)
            gelu(3, 0)
            z_trans(3, 1)
            sq(2, 1)
            gelu(2, 1)
            d_trans(0, 1)
            q_g(1, 0)
            pe_sum(1, 1)
            mm_out0(0, 0)
            d_trans(0, 0)
            stage_one(1, 3)
            mm_out0(0, 2)
            stage_one(1, 0)
            x_trans(1, 1)
            x_trans(1, 0)
            sq(3, 3)
            gelu(3, 3)
            gelu(3, 1)
            sq(3, 1)
            v_dp(1, 1)
            v_dp(1, 3)
            stage_one(1, 2)
            ln(2)
            stage_one(2, 3)
            mm_out0(0, 1)
            ln(3)
            mm_out0(0, 3)
            stage_one(1, 1)
            x_trans(2, 1)
            stage_one(2, 0)
            d_copy("v", 0)
            v_dp(1, 2)
            recip(2)
            q_x(0)
            v_dz(1, 2)
            out0("v", 0, 2)
            x_copy("v", 1)
            out0("v", 0, 1)
            x_trans(2, 0)
            q_x(1)
            gauss(2)
            v_dz(1, 3)
            q_d(0)
            v_dz(1, 0)
            recip(3)
            out0("s", 0, 3)
            x_copy("s", 2)
            v_m("v", 2, 2, 4)
            v_dz(1, 1)
            pe_sum(2, 3)
            pe_sum(2, 2)
            v_m("v", 2, 0, 2)
            pe_sum(2, 0)
            pe_sum(2, 1)
            v_dp(2, 3)
            v_dp(2, 2)
            gauss(3)
            d_trans(1, 0)
            inter("s", 1)
            stage_one(2, 2)
            stage_one(2, 1)
            v_m("v", 3, 0, 2)
            v_dz(2, 3)
            st0(0, 3)
            v_dp(2, 0)
            v_dp(2, 1)
            pe_sum(3, 1)
            d_trans(1, 1)
            v_dz(2, 0)
            v_m("v", 3, 2, 4)
            pe_sum(3, 3)
            pe_sum(3, 2)
            v_dz(2, 2)
            v_dz(2, 1)
            q_o(1)
            mm_out0(1, 1)
            mm_out1(0, 0)
            mm_out0(1, 3)
            stage_one(3, 1)
            stage_one(3, 2)
            out0("s", 0, 0)
            d_copy("s", 1)
            mm_out0(1, 2)
            v_dp(3, 1)
            d_trans(2, 1)
            pe_sum(3, 0)
            v_dp(3, 2)
            v_dp(3, 3)
            d_trans(2, 0)
            out0("s", 1, 1)
            v_dz(3, 1)
            q_x(2)
            stage_one(3, 0)
            out0("s", 1, 3)
            inter("s", 2)
            v_dz(3, 2)
            q_d(1)
            v_dp(3, 0)
            mm_out0(1, 0)
            stage_one(3, 3)
            q_o(2)
            v_dz(3, 0)
            v_dz(3, 3)
            out0("s", 1, 2)
            mm_out0(2, 0)
            d_copy("s", 2)
            x_trans(3, 0)
            x_trans(3, 1)
            mm_out1(1, 0)
            out0("s", 1, 0)
            st0(0, 0)
            q_d(2)
            st0(1, 1)
            inter("v", 3)
            st0(1, 3)
            mm_out0(2, 1)
            mm_out0(2, 2)
            out0("s", 2, 0)
            st0(0, 2)
            st0(0, 1)
            st0(1, 2)
            x_copy("s", 3)
            st0(2, 0)
            st0(1, 0)
            out0("s", 2, 2)
            out0("v", 2, 1)
            d_trans(3, 0)
            d_trans(3, 1)
            mm_out0(2, 3)
            q_o(3)
            mm_out1(2, 0)
            mm_out1(3, 0)
            d_copy("s", 3)
            mm_out0(3, 2, "tr")
            out0("v", 2, 3)
            mm_out1(3, 1)
            mm_out0(3, 0)
            mm_out0(3, 3, "tr")
            out0("s", 3, 2)
            q_x(3)
            q_d(3)
            st0(2, 2)
            out0("s", 3, 0)
            st0(2, 1)
            mm_out1(0, 1)
            mm_out0(3, 1)
            mm_out1(2, 1)
            out0("s", 3, 1)
            mm_out1(3, 2)
            st0(2, 3)
            out0("v", 3, 3)
            mm_out1(3, 3)
            mm_out1(0, 2)
            out1("v", 3)
            mm_out1(0, 3)
            st0(3, 2)
            st0(3, 0)
            mm_out1(2, 2)
            mm_out1(2, 3)
            mm_out1(1, 1)
            st0(3, 3)
            mm_out1(1, 2)
            st0(3, 1)
            mm_out1(1, 3)
            out1("v", 0)
            out1("s", 2)
            st1(3)
            out1("s", 1)
            st1(0)
            st1(2)
            st1(1)
